import numpy as np
import ml_dtypes


def mxq(x, axis, fmt="e4m3"):
    dtype, down = {"e4m3": (ml_dtypes.float8_e4m3fn, 7), "e5m2": (ml_dtypes.float8_e5m2, 14)}[fmt]
    v = np.moveaxis(np.asarray(x, np.float32).astype(ml_dtypes.bfloat16).astype(np.float64), axis, -1)
    blocks = v.reshape(v.shape[:-1] + (-1, 32))
    amax = np.abs(blocks).max(-1, keepdims=True)
    byte = np.maximum(np.where(amax > 0, np.frexp(amax)[1] - 1 + 127, 0) - down, 1)
    scale = np.exp2(byte - 127.0)
    codes = (blocks / scale).astype(np.float32).astype(dtype).astype(np.float64)
    return np.moveaxis((codes * scale).reshape(v.shape), -1, axis)


WIDE = False


def mx_kscale(k):
    if not WIDE:
        return np.ones(k)
    levels = np.array([10, -10, 5, -5, 0])
    a = np.random.permutation(np.resize(levels, k // 512 * 4)).reshape(k // 512, 4)
    idx = np.arange(k)
    return np.exp2(a[idx // 512, idx % 128 // 32])


BF16 = ml_dtypes.bfloat16


def bf(x):
    return np.asarray(x, np.float32).astype(BF16)


def f64(x):
    return np.asarray(x).astype(np.float64)


B, V, D, P, Q, R, O = 16, 16, 512, 512, 512, 1024, 512
NEG_SLOPE = 0.2


def lrelu(v):
    return np.where(v >= 0, v, NEG_SLOPE * v)


def setup_inputs():
    s, u = mx_kscale(Q), mx_kscale(D + R)
    g = np.random.standard_normal((B, V, V, Q)) * 0.8
    return {"h2": bf(lrelu(g) * s),
            "F": bf(np.random.standard_normal((B, V, D)) * u[:D]),
            "W3": bf(np.random.standard_normal((Q, R)) * 1.5 / np.sqrt(Q) / s[:, None] * u[D:]),
            "b3": bf(np.random.standard_normal(R) * 0.3 * u[D:]),
            "Wf": bf(np.random.standard_normal((D + R, O)) / np.sqrt(D + R) / u[:, None]),
            "b_f": bf(np.random.standard_normal(O) * 0.3)}


def reference(h2, F, W3, b3, Wf, b_f):
    h3 = lrelu((mxq(f64(h2), 3, "e4m3") @ mxq(f64(W3), 0, "e4m3")) + f64(b3))
    Msum = h3.sum(axis=-2)
    X = np.concatenate([f64(F), Msum], axis=-1).reshape(-1, D + R)
    return (mxq(X, 1, "e4m3") @ mxq(f64(Wf), 0, "e4m3")) + f64(b_f)

@@ -1,0 +1,260 @@
+import concourse.mybir as mybir
+from concourse.masks import make_identity
+
+F32 = mybir.dt.float32
+BF16 = mybir.dt.bfloat16
+U32 = mybir.dt.uint32
+U8 = mybir.dt.uint8
+FP8X4 = mybir.dt.float8_e4m3fn_x4
+ALU = mybir.AluOpType
+ACT = mybir.ActivationFunctionType
+
+P = 128
+PACK = 4
+VIEWS = 256
+NEIGH = 16
+Q = 512
+R = 1024
+D = 512
+O = 512
+R_TILES = R // P
+CHUNK = 512
+CHUNKS = VIEWS * NEIGH // CHUNK
+J_CHUNK = NEIGH // CHUNKS
+HALVES = VIEWS // P
+K_PASSES = (D + R) // (P * PACK)
+
+FLOPS = 2 * VIEWS * NEIGH * Q * R + 2 * VIEWS * (D + R) * O
+
+
+def regroup(engine_copy, dst, src):
+    engine_copy(
+        out=dst.rearrange("p (c i) t -> p c t i", i=4),
+        in_=src.rearrange("p t (c i) -> p c t i", i=4),
+    )
+
+
+def tile_nonlocalmp_pb_t_kernel(tc, h2, F, W3, b3, Wf, b_f, out):
+    nc = tc.nc
+    h2_v = h2.rearrange("b (q h) j k -> (b q) h j k", h=HALVES)
+    f_v = F.rearrange("b (q h) d -> (b q) h d", h=HALVES)
+    out_v = out.rearrange("(p h) o -> p h o", h=HALVES)
+
+    with tc.tile_pool(name="keep", bufs=1) as keep, tc.tile_pool(name="rows", bufs=8) as rows, tc.tile_pool(
+        name="grp", bufs=3
+    ) as grp, tc.psum_pool(name="work", bufs=4) as work, tc.psum_pool(name="plain", bufs=4) as plain:
+        ident = keep.tile([P, P], F32)
+        w3_raw = keep.tile([P, PACK, R], BF16)
+        w3_grp = keep.tile([P, R, PACK], BF16, align_bytes=64)
+        w3_words = keep.tile([P, R], U32, align_bytes=64)
+        w3_scales = keep.tile([P, R], U8, align_bytes=64)
+        h2_words = keep.tile([P, CHUNKS, CHUNK], U32, align_bytes=64)
+        h2_scales = keep.tile([P, CHUNKS, CHUNK], U8, align_bytes=64)
+        wf_raw = keep.tile([P, K_PASSES, PACK, O], BF16)
+        wf_grp = keep.tile([P, K_PASSES, O, PACK], BF16, align_bytes=64)
+        wf_words = keep.tile([P, K_PASSES, O], U32, align_bytes=64)
+        wf_scales = keep.tile([P, K_PASSES, O], U8, align_bytes=64)
+        x_grp = keep.tile([P, K_PASSES, VIEWS, PACK], BF16, align_bytes=64)
+        x_words = keep.tile([P, K_PASSES, VIEWS], U32, align_bytes=64)
+        x_scales = keep.tile([P, K_PASSES, VIEWS], U8, align_bytes=64)
+        f_sb = keep.tile([P, HALVES, D], BF16)
+        b3_rows = keep.tile([P, P], BF16)
+        b3_rows32 = keep.tile([P, P], F32)
+        neg_b3 = keep.tile([P, R_TILES], F32)
+        ten_b3 = keep.tile([P, R_TILES], F32)
+        bf_all = keep.tile([P, O], BF16)
+        folded = keep.tile([P, R_TILES, VIEWS], F32)
+        result = keep.tile([P, HALVES, O], F32)
+        acc = [keep.tile([P, CHUNK], F32, name="acc%d" % r) for r in range(R_TILES)]
+
+        h2_rows = []
+
+        def load_chunk(c):
+            chunk_rows = rows.tile([P, HALVES, J_CHUNK, Q], BF16, name="chunk_rows")
+            nc.sync.dma_start(out=chunk_rows[:], in_=h2_v[:, :, J_CHUNK * c : J_CHUNK * (c + 1), :])
+            h2_rows.append(chunk_rows)
+
+        nc.vector.memset(b3_rows[:], 0.0)
+        nc.scalar.dma_start(out=b3_rows[0:R_TILES, :], in_=b3.rearrange("(r p) -> r p", p=P))
+        load_chunk(0)
+        for a in range(2):
+            cols = slice(512 * a, 512 * (a + 1))
+            for u in range(2):
+                nc.sync.dma_start(
+                    out=w3_raw[:, 2 * u : 2 * u + 2, cols],
+                    in_=W3[256 * u : 256 * (u + 1), cols].rearrange("(q e) c -> q e c", e=2),
+                )
+        for c in range(1, CHUNKS):
+            load_chunk(c)
+        nc.sync.dma_start(out=f_sb[:], in_=f_v)
+        for u in range(2):
+            nc.sync.dma_start(
+                out=wf_raw[:, 0, 2 * u : 2 * u + 2, :],
+                in_=Wf[256 * u : 256 * (u + 1), :].rearrange("(q e) o -> q e o", e=2),
+            )
+        for g in range(1, K_PASSES):
+            nc.sync.dma_start(
+                out=wf_raw[:, g, :, :],
+                in_=Wf[512 * g : 512 * (g + 1), :].rearrange("(t p) o -> p t o", p=P),
+            )
+        nc.sync.dma_start(out=bf_all[:], in_=b_f.partition_broadcast(P))
+
+        make_identity(nc, ident[:])
+
+        nc.vector.tensor_copy(out=b3_rows32[:], in_=b3_rows[:])
+        b3_t = work.tile([P, CHUNK], F32, tag="work")
+        nc.tensor.transpose(b3_t[:, 0:P], b3_rows32[:], ident[:])
+        nc.vector.tensor_scalar(
+            out=neg_b3[:], in0=b3_t[:, 0:R_TILES], scalar1=-1.0, scalar2=None, op0=ALU.mult
+        )
+        nc.vector.tensor_scalar(
+            out=ten_b3[:], in0=b3_t[:, 0:R_TILES], scalar1=10.0, scalar2=None, op0=ALU.mult
+        )
+
+        for a in range(2):
+            cols = slice(512 * a, 512 * (a + 1))
+            copy = nc.vector.tensor_copy if a == 0 else nc.scalar.copy
+            regroup(copy, w3_grp[:, cols, :], w3_raw[:, :, cols])
+        for a in range(2):
+            cols = slice(512 * a, 512 * (a + 1))
+            nc.vector.quantize_mx(
+                out=w3_words[:, cols].bitcast(FP8X4),
+                scales=w3_scales[:, cols],
+                in_=w3_grp[:, cols, :].rearrange("p c t -> p (c t)"),
+            )
+
+        def transpose_pairs(dst_grp, src_words):
+            xt = work.tile([P, 2, HALVES * P], F32, tag="work")
+            for h in range(HALVES):
+                for u in range(2):
+                    nc.tensor.transpose(
+                        xt[:, u, P * h : P * (h + 1)], src_words[:, h, P * u : P * (u + 1)], ident[:]
+                    )
+            nc.scalar.copy(out=dst_grp.bitcast(F32), in_=xt[:].rearrange("p u c -> p c u"))
+
+        def prepare_chunk(c):
+            chunk_grp = grp.tile([P, CHUNK, PACK], BF16, align_bytes=64, name="chunk_grp")
+            words = h2_rows[c][:].bitcast(F32)
+            for jj in range(J_CHUNK):
+                transpose_pairs(chunk_grp[:, VIEWS * jj : VIEWS * (jj + 1), :], words[:, :, jj, :])
+            nc.vector.quantize_mx(
+                out=h2_words[:, c, :].bitcast(FP8X4),
+                scales=h2_scales[:, c, :],
+                in_=chunk_grp[:].rearrange("p c t -> p (c t)"),
+            )
+
+        def message_pass(dst, r, c, start, stop):
+            tile_cols = slice(P * r, P * (r + 1))
+            nc.tensor.matmul_mx(
+                out=dst,
+                lhsT=w3_words[:, tile_cols].bitcast(FP8X4),
+                lhsT_scale=w3_scales[:, tile_cols],
+                rhs=h2_words[:, c, :].bitcast(FP8X4),
+                rhs_scale=h2_scales[:, c, :],
+                start=start,
+                stop=stop,
+            )
+
+        def relu_sum(r, c, first):
+            bank = work.tile([P, CHUNK], F32, tag="work")
+            message_pass(bank[:], r, c, True, True)
+            if first:
+                nc.vector.tensor_scalar(
+                    out=acc[r][:],
+                    in0=bank[:],
+                    scalar1=neg_b3[:, r : r + 1],
+                    scalar2=ten_b3[:, r : r + 1],
+                    op0=ALU.max,
+                    op1=ALU.add,
+                )
+            else:
+                nc.vector.scalar_tensor_tensor(
+                    out=acc[r][:],
+                    in0=bank[:],
+                    scalar=neg_b3[:, r : r + 1],
+                    in1=acc[r][:],
+                    op0=ALU.max,
+                    op1=ALU.add,
+                )
+
+        def fold(r):
+            nc.vector.tensor_tensor(
+                out=folded[:, r, :], in0=acc[r][:, 0:VIEWS], in1=acc[r][:, VIEWS:CHUNK], op=ALU.add
+            )
+
+        def quantise_x(g):
+            nc.vector.quantize_mx(
+                out=x_words[:, g, :].bitcast(FP8X4),
+                scales=x_scales[:, g, :],
+                in_=x_grp[:, g, :, :].rearrange("p c t -> p (c t)"),
+            )
+
+        def finish_group(g):
+            nc.scalar.activation(
+                out=x_grp[:, g, :, :],
+                in_=folded[:, PACK * (g - 1) : PACK * g, :].rearrange("p t c -> p c t"),
+                func=ACT.Copy,
+                scale=0.8,
+            )
+            quantise_x(g)
+
+        first_half = (0, 1, 2, 3)
+        second_half = (4, 5, 6, 7)
+
+        prepare_chunk(0)
+        prepare_chunk(1)
+        plain_sums = {}
+        for r in second_half:
+            plain_sums[r] = plain.tile([P, CHUNK], F32, name="plain_sum")
+        for c in range(CHUNKS):
+            if c + 2 < CHUNKS:
+                prepare_chunk(c + 2)
+            for r_relu, r_plain in zip(first_half, second_half):
+                relu_sum(r_relu, c, c == 0)
+                message_pass(plain_sums[r_plain][:], r_plain, c, c == 0, c == CHUNKS - 1)
+        for r in second_half:
+            nc.scalar.activation(
+                out=acc[r][:], in_=plain_sums[r][:], func=ACT.Identity, bias=ten_b3[:, r : r + 1], scale=0.25
+            )
+
+        transpose_pairs(x_grp[:, 0, :, :], f_sb[:].bitcast(F32))
+        quantise_x(0)
+        for g in range(K_PASSES):
+            regroup(nc.scalar.copy, wf_grp[:, g, :, :], wf_raw[:, g, :, :])
+            nc.vector.quantize_mx(
+                out=wf_words[:, g, :].bitcast(FP8X4),
+                scales=wf_scales[:, g, :],
+                in_=wf_grp[:, g, :, :].rearrange("p c t -> p (c t)"),
+            )
+
+        for c in range(CHUNKS):
+            if c % 2 == 0:
+                r = first_half[c // 2]
+                plain_sum = plain.tile([P, CHUNK], F32, name="plain_sum")
+                for cc in range(CHUNKS):
+                    message_pass(plain_sum[:], r, cc, cc == 0, cc == CHUNKS - 1)
+                nc.vector.scalar_tensor_tensor(
+                    out=acc[r][:], in0=plain_sum[:], scalar=0.25, in1=acc[r][:], op0=ALU.mult, op1=ALU.add
+                )
+                fold(r)
+            for r in second_half:
+                relu_sum(r, c, False)
+        finish_group(1)
+        for r in second_half:
+            fold(r)
+        finish_group(2)
+
+        for h in range(HALVES):
+            fused = work.tile([P, O], F32, tag="work")
+            for g in range(K_PASSES):
+                nc.tensor.matmul_mx(
+                    out=fused[:],
+                    lhsT=x_words[:, g, P * h : P * (h + 1)].bitcast(FP8X4),
+                    lhsT_scale=x_scales[:, g, P * h : P * (h + 1)],
+                    rhs=wf_words[:, g, :].bitcast(FP8X4),
+                    rhs_scale=wf_scales[:, g, :],
+                    start=(g == 0),
+                    stop=(g == K_PASSES - 1),
+                )
+            nc.vector.tensor_tensor(out=result[:, h, :], in0=fused[:], in1=bf_all[:], op=ALU.add)
+            nc.sync.dma_start(out=out_v[:, h, :], in_=result[:, h, :])

@@ -24,6 +24,8 @@ J_CHUNK = NEIGH // CHUNKS
 HALVES = VIEWS // P
 K_PASSES = (D + R) // (P * PACK)
 
+PLAIN_PER_STEP = 5
+
 FLOPS = 2 * VIEWS * NEIGH * Q * R + 2 * VIEWS * (D + R) * O
 
 
@@ -42,7 +44,9 @@ def tile_nonlocalmp_pb_t_kernel(tc, h2, F, W3, b3, Wf, b_f, out):
 
     with tc.tile_pool(name="keep", bufs=1) as keep, tc.tile_pool(name="rows", bufs=8) as rows, tc.tile_pool(
         name="grp", bufs=3
-    ) as grp, tc.psum_pool(name="work", bufs=4) as work, tc.psum_pool(name="plain", bufs=4) as plain:
+    ) as grp, tc.tile_pool(name="hand", bufs=3) as hand, tc.psum_pool(name="work", bufs=4) as work, tc.psum_pool(
+        name="plain", bufs=4
+    ) as plain:
         ident = keep.tile([P, P], F32)
         w3_raw = keep.tile([P, PACK, R], BF16)
         w3_grp = keep.tile([P, R, PACK], BF16, align_bytes=64)
@@ -60,8 +64,9 @@ def tile_nonlocalmp_pb_t_kernel(tc, h2, F, W3, b3, Wf, b_f, out):
         f_sb = keep.tile([P, HALVES, D], BF16)
         b3_rows = keep.tile([P, P], BF16)
         b3_rows32 = keep.tile([P, P], F32)
+        b3_col = keep.tile([P, R_TILES], F32)
         neg_b3 = keep.tile([P, R_TILES], F32)
-        ten_b3 = keep.tile([P, R_TILES], F32)
+        fold_b3 = keep.tile([P, R_TILES], F32)
         bf_all = keep.tile([P, O], BF16)
         folded = keep.tile([P, R_TILES, VIEWS], F32)
         result = keep.tile([P, HALVES, O], F32)
@@ -104,11 +109,11 @@ def tile_nonlocalmp_pb_t_kernel(tc, h2, F, W3, b3, Wf, b_f, out):
         nc.vector.tensor_copy(out=b3_rows32[:], in_=b3_rows[:])
         b3_t = work.tile([P, CHUNK], F32, tag="work")
         nc.tensor.transpose(b3_t[:, 0:P], b3_rows32[:], ident[:])
+        nc.vector.tensor_copy(out=b3_col[:], in_=b3_t[:, 0:R_TILES])
+        nc.vector.tensor_scalar(out=neg_b3[:], in0=b3_col[:], scalar1=-1.0, scalar2=None, op0=ALU.mult)
+        nc.vector.tensor_scalar(out=fold_b3[:], in0=b3_col[:], scalar1=20.0, scalar2=None, op0=ALU.mult)
         nc.vector.tensor_scalar(
-            out=neg_b3[:], in0=b3_t[:, 0:R_TILES], scalar1=-1.0, scalar2=None, op0=ALU.mult
-        )
-        nc.vector.tensor_scalar(
-            out=ten_b3[:], in0=b3_t[:, 0:R_TILES], scalar1=10.0, scalar2=None, op0=ALU.mult
+            out=fold_b3[:, 0:R_TILES:4], in0=b3_col[:, 0:R_TILES:4], scalar1=4.0, scalar2=None, op0=ALU.mult
         )
 
         for a in range(2):
@@ -158,14 +163,16 @@ def tile_nonlocalmp_pb_t_kernel(tc, h2, F, W3, b3, Wf, b_f, out):
         def relu_sum(r, c, first):
             bank = work.tile([P, CHUNK], F32, tag="work")
             message_pass(bank[:], r, c, True, True)
-            if first:
+            if r % 4 == 0:
+                if first:
+                    nc.scalar.activation(out=acc[r][:], in_=bank[:], func=ACT.Relu, bias=b3_col[:, r : r + 1])
+                else:
+                    relu_sb = hand.tile([P, CHUNK], F32, tag="hand")
+                    nc.scalar.activation(out=relu_sb[:], in_=bank[:], func=ACT.Relu, bias=b3_col[:, r : r + 1])
+                    nc.gpsimd.tensor_tensor(out=acc[r][:], in0=acc[r][:], in1=relu_sb[:], op=ALU.add)
+            elif first:
                 nc.vector.tensor_scalar(
-                    out=acc[r][:],
-                    in0=bank[:],
-                    scalar1=neg_b3[:, r : r + 1],
-                    scalar2=ten_b3[:, r : r + 1],
-                    op0=ALU.max,
-                    op1=ALU.add,
+                    out=acc[r][:], in0=bank[:], scalar1=neg_b3[:, r : r + 1], scalar2=None, op0=ALU.max
                 )
             else:
                 nc.vector.scalar_tensor_tensor(
@@ -178,28 +185,36 @@ def tile_nonlocalmp_pb_t_kernel(tc, h2, F, W3, b3, Wf, b_f, out):
                 )
 
         def fold(r):
-            nc.vector.tensor_tensor(
-                out=folded[:, r, :], in0=acc[r][:, 0:VIEWS], in1=acc[r][:, VIEWS:CHUNK], op=ALU.add
+            nc.vector.scalar_tensor_tensor(
+                out=folded[:, r, :],
+                in0=acc[r][:, 0:VIEWS],
+                scalar=fold_b3[:, r : r + 1],
+                in1=acc[r][:, VIEWS:CHUNK],
+                op0=ALU.add,
+                op1=ALU.add,
             )
 
-        def quantise_x(g):
+        def quantise_x(g, cols):
             nc.vector.quantize_mx(
-                out=x_words[:, g, :].bitcast(FP8X4),
-                scales=x_scales[:, g, :],
-                in_=x_grp[:, g, :, :].rearrange("p c t -> p (c t)"),
+                out=x_words[:, g, cols].bitcast(FP8X4),
+                scales=x_scales[:, g, cols],
+                in_=x_grp[:, g, cols, :].rearrange("p c t -> p (c t)"),
             )
 
-        def finish_group(g):
-            nc.scalar.activation(
-                out=x_grp[:, g, :, :],
-                in_=folded[:, PACK * (g - 1) : PACK * g, :].rearrange("p t c -> p c t"),
-                func=ACT.Copy,
-                scale=0.8,
+        def fusion_pass(fused, h, g):
+            nc.tensor.matmul_mx(
+                out=fused[:],
+                lhsT=x_words[:, g, P * h : P * (h + 1)].bitcast(FP8X4),
+                lhsT_scale=x_scales[:, g, P * h : P * (h + 1)],
+                rhs=wf_words[:, g, :].bitcast(FP8X4),
+                rhs_scale=wf_scales[:, g, :],
+                start=(g == 0),
+                stop=(g == K_PASSES - 1),
             )
-            quantise_x(g)
 
         first_half = (0, 1, 2, 3)
         second_half = (4, 5, 6, 7)
+        all_views = slice(0, VIEWS)
 
         prepare_chunk(0)
         prepare_chunk(1)
@@ -212,49 +227,72 @@ def tile_nonlocalmp_pb_t_kernel(tc, h2, F, W3, b3, Wf, b_f, out):
             for r_relu, r_plain in zip(first_half, second_half):
                 relu_sum(r_relu, c, c == 0)
                 message_pass(plain_sums[r_plain][:], r_plain, c, c == 0, c == CHUNKS - 1)
+            if c % 2 == 1 and c // 2 < K_PASSES:
+                g = c // 2
+                regroup(nc.scalar.copy, wf_grp[:, g, :, :], wf_raw[:, g, :, :])
+                nc.vector.quantize_mx(
+                    out=wf_words[:, g, :].bitcast(FP8X4),
+                    scales=wf_scales[:, g, :],
+                    in_=wf_grp[:, g, :, :].rearrange("p c t -> p (c t)"),
+                )
         for r in second_half:
-            nc.scalar.activation(
-                out=acc[r][:], in_=plain_sums[r][:], func=ACT.Identity, bias=ten_b3[:, r : r + 1], scale=0.25
-            )
-
+            nc.scalar.activation(out=acc[r][:], in_=plain_sums[r][:], func=ACT.Copy, scale=0.25)
         transpose_pairs(x_grp[:, 0, :, :], f_sb[:].bitcast(F32))
-        quantise_x(0)
-        for g in range(K_PASSES):
-            regroup(nc.scalar.copy, wf_grp[:, g, :, :], wf_raw[:, g, :, :])
-            nc.vector.quantize_mx(
-                out=wf_words[:, g, :].bitcast(FP8X4),
-                scales=wf_scales[:, g, :],
-                in_=wf_grp[:, g, :, :].rearrange("p c t -> p (c t)"),
-            )
+        quantise_x(0, all_views)
+
+        n_plain = len(first_half) * CHUNKS
+        to_fold = []
+        fused = []
+
+        def finish_first_half(r):
+            fold(r)
+            if r == first_half[-1]:
+                nc.scalar.activation(
+                    out=x_grp[:, 1, :, :],
+                    in_=folded[:, 0:PACK, :].rearrange("p t c -> p c t"),
+                    func=ACT.Copy,
+                    scale=0.8,
+                )
+                quantise_x(1, all_views)
+                for h in range(HALVES):
+                    fused.append(plain.tile([P, O], F32, name="plain_sum"))
+                    fusion_pass(fused[h], h, 0)
+                    fusion_pass(fused[h], h, 1)
 
         for c in range(CHUNKS):
-            if c % 2 == 0:
-                r = first_half[c // 2]
-                plain_sum = plain.tile([P, CHUNK], F32, name="plain_sum")
-                for cc in range(CHUNKS):
-                    message_pass(plain_sum[:], r, cc, cc == 0, cc == CHUNKS - 1)
-                nc.vector.scalar_tensor_tensor(
-                    out=acc[r][:], in0=plain_sum[:], scalar=0.25, in1=acc[r][:], op0=ALU.mult, op1=ALU.add
-                )
-                fold(r)
-            for r in second_half:
-                relu_sum(r, c, False)
-        finish_group(1)
+            for r in to_fold:
+                finish_first_half(r)
+            to_fold = []
+            for i in range(PLAIN_PER_STEP):
+                if i < len(second_half):
+                    relu_sum(second_half[i], c, False)
+                n = PLAIN_PER_STEP * c + i
+                if n < n_plain:
+                    r = first_half[n // CHUNKS]
+                    cc = n % CHUNKS
+                    if cc == 0:
+                        plain_sums[r] = plain.tile([P, CHUNK], F32, name="plain_sum")
+                    message_pass(plain_sums[r][:], r, cc, cc == 0, cc == CHUNKS - 1)
+                    if cc == CHUNKS - 1:
+                        plain_sb = hand.tile([P, CHUNK], F32, tag="hand")
+                        nc.scalar.activation(out=plain_sb[:], in_=plain_sums[r][:], func=ACT.Copy, scale=0.25)
+                        nc.gpsimd.tensor_tensor(out=acc[r][:], in0=acc[r][:], in1=plain_sb[:], op=ALU.add)
+                        to_fold.append(r)
+
+        for r in to_fold:
+            finish_first_half(r)
+
         for r in second_half:
             fold(r)
-        finish_group(2)
-
         for h in range(HALVES):
-            fused = work.tile([P, O], F32, tag="work")
-            for g in range(K_PASSES):
-                nc.tensor.matmul_mx(
-                    out=fused[:],
-                    lhsT=x_words[:, g, P * h : P * (h + 1)].bitcast(FP8X4),
-                    lhsT_scale=x_scales[:, g, P * h : P * (h + 1)],
-                    rhs=wf_words[:, g, :].bitcast(FP8X4),
-                    rhs_scale=wf_scales[:, g, :],
-                    start=(g == 0),
-                    stop=(g == K_PASSES - 1),
-                )
-            nc.vector.tensor_tensor(out=result[:, h, :], in0=fused[:], in1=bf_all[:], op=ALU.add)
+            cols = slice(P * h, P * (h + 1))
+            src = folded[:, PACK : 2 * PACK, cols].rearrange("p t c -> p c t")
+            if h == 0:
+                nc.scalar.activation(out=x_grp[:, 2, cols, :], in_=src, func=ACT.Copy, scale=0.8)
+            else:
+                nc.vector.tensor_scalar(out=x_grp[:, 2, cols, :], in0=src, scalar1=0.8, scalar2=None, op0=ALU.mult)
+        for h in range(HALVES):
+            quantise_x(2, slice(P * h, P * (h + 1)))
+            fusion_pass(fused[h], h, 2)
+            nc.vector.tensor_tensor(out=result[:, h, :], in0=fused[h][:], in1=bf_all[:], op=ALU.add)
             nc.sync.dma_start(out=out_v[:, h, :], in_=result[:, h, :])

@@ -23,8 +23,12 @@ CHUNKS = VIEWS * NEIGH // CHUNK
 J_CHUNK = NEIGH // CHUNKS
 HALVES = VIEWS // P
 K_PASSES = (D + R) // (P * PACK)
+W3_BLOCK = 256
+W3_BLOCKS = R // W3_BLOCK
 
-PLAIN_PER_STEP = 5
+EARLY_TILES = 5
+EARLY_BLOCKS = 3
+PLAIN_PER_STEP = 8
 
 FLOPS = 2 * VIEWS * NEIGH * Q * R + 2 * VIEWS * (D + R) * O
 
@@ -36,17 +40,28 @@ def regroup(engine_copy, dst, src):
     )
 
 
+def share(items, i, n):
+    return items[len(items) * i // n : len(items) * (i + 1) // n]
+
+
+def through_scalar(r):
+    return r % 3 == 1
+
+
 def tile_nonlocalmp_pb_t_kernel(tc, h2, F, W3, b3, Wf, b_f, out):
     nc = tc.nc
     h2_v = h2.rearrange("b (q h) j k -> (b q) h j k", h=HALVES)
     f_v = F.rearrange("b (q h) d -> (b q) h d", h=HALVES)
     out_v = out.rearrange("(p h) o -> p h o", h=HALVES)
 
-    with tc.tile_pool(name="keep", bufs=1) as keep, tc.tile_pool(name="rows", bufs=8) as rows, tc.tile_pool(
+    early = list(range(EARLY_TILES))
+    late = list(range(EARLY_TILES, R_TILES))
+
+    with tc.tile_pool(name="keep", bufs=1) as keep, tc.tile_pool(name="rows", bufs=CHUNKS) as rows, tc.tile_pool(
         name="grp", bufs=3
-    ) as grp, tc.tile_pool(name="hand", bufs=3) as hand, tc.psum_pool(name="work", bufs=4) as work, tc.psum_pool(
-        name="plain", bufs=4
-    ) as plain:
+    ) as grp, tc.tile_pool(name="hand", bufs=4) as hand, tc.psum_pool(
+        name="work", bufs=8 - len(late)
+    ) as work, tc.psum_pool(name="plain", bufs=len(late)) as plain, tc.manual_schedule():
         ident = keep.tile([P, P], F32)
         w3_raw = keep.tile([P, PACK, R], BF16)
         w3_grp = keep.tile([P, R, PACK], BF16, align_bytes=64)
@@ -79,17 +94,23 @@ def tile_nonlocalmp_pb_t_kernel(tc, h2, F, W3, b3, Wf, b_f, out):
             nc.sync.dma_start(out=chunk_rows[:], in_=h2_v[:, :, J_CHUNK * c : J_CHUNK * (c + 1), :])
             h2_rows.append(chunk_rows)
 
-        nc.vector.memset(b3_rows[:], 0.0)
-        nc.scalar.dma_start(out=b3_rows[0:R_TILES, :], in_=b3.rearrange("(r p) -> r p", p=P))
-        load_chunk(0)
-        for a in range(2):
-            cols = slice(512 * a, 512 * (a + 1))
+        def load_w3(block):
+            cols = slice(W3_BLOCK * block, W3_BLOCK * (block + 1))
             for u in range(2):
                 nc.sync.dma_start(
                     out=w3_raw[:, 2 * u : 2 * u + 2, cols],
                     in_=W3[256 * u : 256 * (u + 1), cols].rearrange("(q e) c -> q e c", e=2),
                 )
-        for c in range(1, CHUNKS):
+
+        nc.vector.memset(b3_rows[:], 0.0)
+        nc.scalar.dma_start(out=b3_rows[0:R_TILES, :], in_=b3.rearrange("(r p) -> r p", p=P))
+        load_chunk(0)
+        for block in range(EARLY_BLOCKS):
+            load_w3(block)
+        load_chunk(1)
+        for block in range(EARLY_BLOCKS, W3_BLOCKS):
+            load_w3(block)
+        for c in range(2, CHUNKS):
             load_chunk(c)
         nc.sync.dma_start(out=f_sb[:], in_=f_v)
         for u in range(2):
@@ -105,28 +126,8 @@ def tile_nonlocalmp_pb_t_kernel(tc, h2, F, W3, b3, Wf, b_f, out):
         nc.sync.dma_start(out=bf_all[:], in_=b_f.partition_broadcast(P))
 
         make_identity(nc, ident[:])
-
-        nc.vector.tensor_copy(out=b3_rows32[:], in_=b3_rows[:])
-        b3_t = work.tile([P, CHUNK], F32, tag="work")
-        nc.tensor.transpose(b3_t[:, 0:P], b3_rows32[:], ident[:])
-        nc.vector.tensor_copy(out=b3_col[:], in_=b3_t[:, 0:R_TILES])
-        nc.vector.tensor_scalar(out=neg_b3[:], in0=b3_col[:], scalar1=-1.0, scalar2=None, op0=ALU.mult)
-        nc.vector.tensor_scalar(out=fold_b3[:], in0=b3_col[:], scalar1=20.0, scalar2=None, op0=ALU.mult)
-        nc.vector.tensor_scalar(
-            out=fold_b3[:, 0:R_TILES:4], in0=b3_col[:, 0:R_TILES:4], scalar1=4.0, scalar2=None, op0=ALU.mult
-        )
-
-        for a in range(2):
-            cols = slice(512 * a, 512 * (a + 1))
-            copy = nc.vector.tensor_copy if a == 0 else nc.scalar.copy
-            regroup(copy, w3_grp[:, cols, :], w3_raw[:, :, cols])
-        for a in range(2):
-            cols = slice(512 * a, 512 * (a + 1))
-            nc.vector.quantize_mx(
-                out=w3_words[:, cols].bitcast(FP8X4),
-                scales=w3_scales[:, cols],
-                in_=w3_grp[:, cols, :].rearrange("p c t -> p (c t)"),
-            )
+        for r in late:
+            nc.gpsimd.memset(acc[r][:, VIEWS:CHUNK], 0.0)
 
         def transpose_pairs(dst_grp, src_words):
             xt = work.tile([P, 2, HALVES * P], F32, tag="work")
@@ -137,33 +138,49 @@ def tile_nonlocalmp_pb_t_kernel(tc, h2, F, W3, b3, Wf, b_f, out):
                     )
             nc.scalar.copy(out=dst_grp.bitcast(F32), in_=xt[:].rearrange("p u c -> p c u"))
 
-        def prepare_chunk(c):
-            chunk_grp = grp.tile([P, CHUNK, PACK], BF16, align_bytes=64, name="chunk_grp")
+        chunk_grps = {}
+
+        def transpose_chunk(c):
+            chunk_grps[c] = grp.tile([P, CHUNK, PACK], BF16, align_bytes=64, name="chunk_grp")
             words = h2_rows[c][:].bitcast(F32)
             for jj in range(J_CHUNK):
-                transpose_pairs(chunk_grp[:, VIEWS * jj : VIEWS * (jj + 1), :], words[:, :, jj, :])
+                transpose_pairs(chunk_grps[c][:, VIEWS * jj : VIEWS * (jj + 1), :], words[:, :, jj, :])
+
+        def quantise_chunk(c):
             nc.vector.quantize_mx(
                 out=h2_words[:, c, :].bitcast(FP8X4),
                 scales=h2_scales[:, c, :],
-                in_=chunk_grp[:].rearrange("p c t -> p (c t)"),
+                in_=chunk_grps[c][:].rearrange("p c t -> p (c t)"),
             )
 
-        def message_pass(dst, r, c, start, stop):
+        def regroup_w3(engine_copy, block):
+            cols = slice(W3_BLOCK * block, W3_BLOCK * (block + 1))
+            regroup(engine_copy, w3_grp[:, cols, :], w3_raw[:, :, cols])
+
+        def quantise_w3(block):
+            cols = slice(W3_BLOCK * block, W3_BLOCK * (block + 1))
+            nc.vector.quantize_mx(
+                out=w3_words[:, cols].bitcast(FP8X4),
+                scales=w3_scales[:, cols],
+                in_=w3_grp[:, cols, :].rearrange("p c t -> p (c t)"),
+            )
+
+        def message_pass(dst, r, c, cols, start, stop):
             tile_cols = slice(P * r, P * (r + 1))
             nc.tensor.matmul_mx(
                 out=dst,
                 lhsT=w3_words[:, tile_cols].bitcast(FP8X4),
                 lhsT_scale=w3_scales[:, tile_cols],
-                rhs=h2_words[:, c, :].bitcast(FP8X4),
-                rhs_scale=h2_scales[:, c, :],
+                rhs=h2_words[:, c, cols].bitcast(FP8X4),
+                rhs_scale=h2_scales[:, c, cols],
                 start=start,
                 stop=stop,
             )
 
         def relu_sum(r, c, first):
             bank = work.tile([P, CHUNK], F32, tag="work")
-            message_pass(bank[:], r, c, True, True)
-            if r % 4 == 0:
+            message_pass(bank[:], r, c, slice(0, CHUNK), True, True)
+            if through_scalar(r):
                 if first:
                     nc.scalar.activation(out=acc[r][:], in_=bank[:], func=ACT.Relu, bias=b3_col[:, r : r + 1])
                 else:
@@ -184,6 +201,21 @@ def tile_nonlocalmp_pb_t_kernel(tc, h2, F, W3, b3, Wf, b_f, out):
                     op1=ALU.add,
                 )
 
+        plain_sums = {}
+
+        def plain_pass(r, j):
+            if j == 0:
+                plain_sums[r] = plain.tile([P, CHUNK], F32, name="plain_sum")
+            jj = j % J_CHUNK
+            message_pass(
+                plain_sums[r][:, 0:VIEWS],
+                r,
+                j // J_CHUNK,
+                slice(VIEWS * jj, VIEWS * (jj + 1)),
+                j == 0,
+                j == NEIGH - 1,
+            )
+
         def fold(r):
             nc.vector.scalar_tensor_tensor(
                 out=folded[:, r, :],
@@ -193,6 +225,39 @@ def tile_nonlocalmp_pb_t_kernel(tc, h2, F, W3, b3, Wf, b_f, out):
                 op0=ALU.add,
                 op1=ALU.add,
             )
+
+        def add_plain_sum(r):
+            nc.vector.scalar_tensor_tensor(
+                out=folded[:, r, :],
+                in0=plain_sums[r][:, 0:VIEWS],
+                scalar=0.25,
+                in1=folded[:, r, :],
+                op0=ALU.mult,
+                op1=ALU.add,
+            )
+
+        def regroup_wf(piece):
+            g = piece // 2
+            cols = slice((O // 2) * (piece % 2), (O // 2) * (piece % 2 + 1))
+            regroup(nc.scalar.copy, wf_grp[:, g, cols, :], wf_raw[:, g, :, cols])
+
+        def quantise_wf(g):
+            nc.vector.quantize_mx(
+                out=wf_words[:, g, :].bitcast(FP8X4),
+                scales=wf_scales[:, g, :],
+                in_=wf_grp[:, g, :, :].rearrange("p c t -> p (c t)"),
+            )
+
+        def regroup_x(g):
+            for h in range(HALVES):
+                cols = slice(P * h, P * (h + 1))
+                src = folded[:, PACK * (g - 1) : PACK * g, cols].rearrange("p t c -> p c t")
+                if h == 0:
+                    nc.vector.tensor_scalar(
+                        out=x_grp[:, g, cols, :], in0=src, scalar1=0.8, scalar2=None, op0=ALU.mult
+                    )
+                else:
+                    nc.scalar.activation(out=x_grp[:, g, cols, :], in_=src, func=ACT.Copy, scale=0.8)
 
         def quantise_x(g, cols):
             nc.vector.quantize_mx(
@@ -212,85 +277,79 @@ def tile_nonlocalmp_pb_t_kernel(tc, h2, F, W3, b3, Wf, b_f, out):
                 stop=(g == K_PASSES - 1),
             )
 
-        first_half = (0, 1, 2, 3)
-        second_half = (4, 5, 6, 7)
-        all_views = slice(0, VIEWS)
+        transpose_chunk(0)
+        nc.vector.tensor_copy(out=b3_rows32[:], in_=b3_rows[:])
+        b3_t = work.tile([P, CHUNK], F32, tag="work")
+        nc.tensor.transpose(b3_t[:, 0:P], b3_rows32[:], ident[:])
+        regroup_w3(nc.vector.tensor_copy, 0)
+        regroup_w3(nc.scalar.copy, 1)
+        quantise_chunk(0)
+        quantise_w3(0)
+        nc.vector.tensor_copy(out=b3_col[:], in_=b3_t[:, 0:R_TILES])
+        nc.vector.tensor_scalar(out=neg_b3[:], in0=b3_col[:], scalar1=-1.0, scalar2=None, op0=ALU.mult)
+        nc.vector.tensor_scalar(out=fold_b3[:], in0=b3_col[:], scalar1=20.0, scalar2=None, op0=ALU.mult)
+        nc.vector.tensor_scalar(
+            out=fold_b3[:, 1:R_TILES:3], in0=b3_col[:, 1:R_TILES:3], scalar1=4.0, scalar2=None, op0=ALU.mult
+        )
+        regroup_w3(nc.vector.tensor_copy, 2)
+        quantise_w3(1)
+        quantise_w3(2)
 
-        prepare_chunk(0)
-        prepare_chunk(1)
-        plain_sums = {}
-        for r in second_half:
-            plain_sums[r] = plain.tile([P, CHUNK], F32, name="plain_sum")
         for c in range(CHUNKS):
+            behind = [(r, J_CHUNK * (c - 1) + jj) for r in late for jj in range(J_CHUNK)] if c > 0 else []
+            for i, r in enumerate(early):
+                relu_sum(r, c, c == 0)
+                for r_plain, j in share(behind, i, len(early)):
+                    plain_pass(r_plain, j)
+                if i == 1 and c == 0:
+                    transpose_chunk(1)
+                if i == 1 and 0 < c < CHUNKS - 1:
+                    quantise_chunk(c + 1)
+            if c == 0:
+                regroup_w3(nc.vector.tensor_copy, 3)
+                quantise_chunk(1)
+                quantise_w3(3)
             if c + 2 < CHUNKS:
-                prepare_chunk(c + 2)
-            for r_relu, r_plain in zip(first_half, second_half):
-                relu_sum(r_relu, c, c == 0)
-                message_pass(plain_sums[r_plain][:], r_plain, c, c == 0, c == CHUNKS - 1)
-            if c % 2 == 1 and c // 2 < K_PASSES:
-                g = c // 2
-                regroup(nc.scalar.copy, wf_grp[:, g, :, :], wf_raw[:, g, :, :])
-                nc.vector.quantize_mx(
-                    out=wf_words[:, g, :].bitcast(FP8X4),
-                    scales=wf_scales[:, g, :],
-                    in_=wf_grp[:, g, :, :].rearrange("p c t -> p (c t)"),
-                )
-        for r in second_half:
-            nc.scalar.activation(out=acc[r][:], in_=plain_sums[r][:], func=ACT.Copy, scale=0.25)
-        transpose_pairs(x_grp[:, 0, :, :], f_sb[:].bitcast(F32))
-        quantise_x(0, all_views)
+                transpose_chunk(c + 2)
+            if c + 2 == CHUNKS:
+                transpose_pairs(x_grp[:, 0, :, :], f_sb[:].bitcast(F32))
+            if c + 1 == CHUNKS:
+                quantise_x(0, slice(0, VIEWS))
+        for r in late:
+            for jj in range(J_CHUNK):
+                plain_pass(r, NEIGH - J_CHUNK + jj)
+            nc.scalar.activation(out=acc[r][:, 0:VIEWS], in_=plain_sums[r][:, 0:VIEWS], func=ACT.Copy, scale=0.25)
 
-        n_plain = len(first_half) * CHUNKS
-        to_fold = []
-        fused = []
-
-        def finish_first_half(r):
-            fold(r)
-            if r == first_half[-1]:
-                nc.scalar.activation(
-                    out=x_grp[:, 1, :, :],
-                    in_=folded[:, 0:PACK, :].rearrange("p t c -> p c t"),
-                    func=ACT.Copy,
-                    scale=0.8,
-                )
-                quantise_x(1, all_views)
-                for h in range(HALVES):
-                    fused.append(plain.tile([P, O], F32, name="plain_sum"))
-                    fusion_pass(fused[h], h, 0)
-                    fusion_pass(fused[h], h, 1)
-
+        early_plain = [(r, j) for r in early for j in range(NEIGH)]
         for c in range(CHUNKS):
-            for r in to_fold:
-                finish_first_half(r)
-            to_fold = []
-            for i in range(PLAIN_PER_STEP):
-                if i < len(second_half):
-                    relu_sum(second_half[i], c, False)
-                n = PLAIN_PER_STEP * c + i
-                if n < n_plain:
-                    r = first_half[n // CHUNKS]
-                    cc = n % CHUNKS
-                    if cc == 0:
-                        plain_sums[r] = plain.tile([P, CHUNK], F32, name="plain_sum")
-                    message_pass(plain_sums[r][:], r, cc, cc == 0, cc == CHUNKS - 1)
-                    if cc == CHUNKS - 1:
-                        plain_sb = hand.tile([P, CHUNK], F32, tag="hand")
-                        nc.scalar.activation(out=plain_sb[:], in_=plain_sums[r][:], func=ACT.Copy, scale=0.25)
-                        nc.gpsimd.tensor_tensor(out=acc[r][:], in0=acc[r][:], in1=plain_sb[:], op=ALU.add)
-                        to_fold.append(r)
+            step_plain = early_plain[PLAIN_PER_STEP * c : PLAIN_PER_STEP * (c + 1)]
+            for i, r in enumerate(late):
+                relu_sum(r, c, False)
+                for r_plain, j in share(step_plain, i, len(late)):
+                    plain_pass(r_plain, j)
+            if c < len(early):
+                fold(early[c])
+            for r_plain, j in step_plain:
+                if j == NEIGH - 1:
+                    add_plain_sum(r_plain)
+            if c < 2 * K_PASSES:
+                regroup_wf(c)
+            if c >= 2 and c % 2 == 0:
+                quantise_wf(c // 2 - 1)
 
-        for r in to_fold:
-            finish_first_half(r)
-
-        for r in second_half:
+        for r_plain, j in early_plain[PLAIN_PER_STEP * CHUNKS :]:
+            plain_pass(r_plain, j)
+        regroup_x(1)
+        for r in late:
             fold(r)
+        quantise_x(1, slice(0, VIEWS))
+        fused = []
         for h in range(HALVES):
-            cols = slice(P * h, P * (h + 1))
-            src = folded[:, PACK : 2 * PACK, cols].rearrange("p t c -> p c t")
-            if h == 0:
-                nc.scalar.activation(out=x_grp[:, 2, cols, :], in_=src, func=ACT.Copy, scale=0.8)
-            else:
-                nc.vector.tensor_scalar(out=x_grp[:, 2, cols, :], in0=src, scalar1=0.8, scalar2=None, op0=ALU.mult)
+            fused.append(work.tile([P, O], F32, tag="work", name="fused"))
+            fusion_pass(fused[h], h, 0)
+            fusion_pass(fused[h], h, 1)
+        add_plain_sum(early[-1])
+        regroup_x(2)
         for h in range(HALVES):
             quantise_x(2, slice(P * h, P * (h + 1)))
             fusion_pass(fused[h], h, 2)

@@ -24,11 +24,13 @@ J_CHUNK = NEIGH // CHUNKS
 HALVES = VIEWS // P
 K_PASSES = (D + R) // (P * PACK)
 W3_BLOCK = 256
-W3_BLOCKS = R // W3_BLOCK
 
-EARLY_TILES = 5
-EARLY_BLOCKS = 3
-PLAIN_PER_STEP = 8
+PAIRS = [(0, 1), (2, 3), (4, 5), (6, 7)]
+LAST = R_TILES - 1
+MIXED = R_TILES - 2
+VECTOR_START = 2
+MIXED_HALF = CHUNKS // 2
+LAST_STEP_COLUMNS = 5 * P
 
 FLOPS = 2 * VIEWS * NEIGH * Q * R + 2 * VIEWS * (D + R) * O
 
@@ -40,12 +42,10 @@ def regroup(engine_copy, dst, src):
     )
 
 
-def share(items, i, n):
-    return items[len(items) * i // n : len(items) * (i + 1) // n]
-
-
-def through_scalar(r):
-    return r % 3 == 1
+def through_scalar(r, c):
+    if r == MIXED:
+        return c < MIXED_HALF
+    return r % 2 == 1 and r != LAST and c >= VECTOR_START
 
 
 def tile_nonlocalmp_pb_t_kernel(tc, h2, F, W3, b3, Wf, b_f, out):
@@ -54,16 +54,14 @@ def tile_nonlocalmp_pb_t_kernel(tc, h2, F, W3, b3, Wf, b_f, out):
     f_v = F.rearrange("b (q h) d -> (b q) h d", h=HALVES)
     out_v = out.rearrange("(p h) o -> p h o", h=HALVES)
 
-    early = list(range(EARLY_TILES))
-    late = list(range(EARLY_TILES, R_TILES))
-
     with tc.tile_pool(name="keep", bufs=1) as keep, tc.tile_pool(name="rows", bufs=CHUNKS) as rows, tc.tile_pool(
         name="grp", bufs=3
     ) as grp, tc.tile_pool(name="hand", bufs=4) as hand, tc.psum_pool(
-        name="work", bufs=8 - len(late)
-    ) as work, tc.psum_pool(name="plain", bufs=len(late)) as plain, tc.manual_schedule():
+        name="work", bufs=6
+    ) as work, tc.psum_pool(name="plain", bufs=2) as plain, tc.manual_schedule():
         ident = keep.tile([P, P], F32)
-        w3_raw = keep.tile([P, PACK, R], BF16)
+        w3_first = keep.tile([P, PACK, W3_BLOCK], BF16)
+        w3_rest = keep.tile([P, PACK, R - W3_BLOCK], BF16)
         w3_grp = keep.tile([P, R, PACK], BF16, align_bytes=64)
         w3_words = keep.tile([P, R], U32, align_bytes=64)
         w3_scales = keep.tile([P, R], U8, align_bytes=64)
@@ -86,6 +84,7 @@ def tile_nonlocalmp_pb_t_kernel(tc, h2, F, W3, b3, Wf, b_f, out):
         folded = keep.tile([P, R_TILES, VIEWS], F32)
         result = keep.tile([P, HALVES, O], F32)
         acc = [keep.tile([P, CHUNK], F32, name="acc%d" % r) for r in range(R_TILES)]
+        mixed_acc = keep.tile([P, CHUNK], F32)
 
         h2_rows = []
 
@@ -94,24 +93,20 @@ def tile_nonlocalmp_pb_t_kernel(tc, h2, F, W3, b3, Wf, b_f, out):
             nc.sync.dma_start(out=chunk_rows[:], in_=h2_v[:, :, J_CHUNK * c : J_CHUNK * (c + 1), :])
             h2_rows.append(chunk_rows)
 
-        def load_w3(block):
-            cols = slice(W3_BLOCK * block, W3_BLOCK * (block + 1))
+        def load_w3(raw, cols):
             for u in range(2):
                 nc.sync.dma_start(
-                    out=w3_raw[:, 2 * u : 2 * u + 2, cols],
+                    out=raw[:, 2 * u : 2 * u + 2, :],
                     in_=W3[256 * u : 256 * (u + 1), cols].rearrange("(q e) c -> q e c", e=2),
                 )
 
         nc.vector.memset(b3_rows[:], 0.0)
         nc.scalar.dma_start(out=b3_rows[0:R_TILES, :], in_=b3.rearrange("(r p) -> r p", p=P))
         load_chunk(0)
-        for block in range(EARLY_BLOCKS):
-            load_w3(block)
-        load_chunk(1)
-        for block in range(EARLY_BLOCKS, W3_BLOCKS):
-            load_w3(block)
-        for c in range(2, CHUNKS):
+        load_w3(w3_first, slice(0, W3_BLOCK))
+        for c in range(1, CHUNKS):
             load_chunk(c)
+        load_w3(w3_rest, slice(W3_BLOCK, R))
         nc.sync.dma_start(out=f_sb[:], in_=f_v)
         for u in range(2):
             nc.sync.dma_start(
@@ -126,8 +121,6 @@ def tile_nonlocalmp_pb_t_kernel(tc, h2, F, W3, b3, Wf, b_f, out):
         nc.sync.dma_start(out=bf_all[:], in_=b_f.partition_broadcast(P))
 
         make_identity(nc, ident[:])
-        for r in late:
-            nc.gpsimd.memset(acc[r][:, VIEWS:CHUNK], 0.0)
 
         def transpose_pairs(dst_grp, src_words):
             xt = work.tile([P, 2, HALVES * P], F32, tag="work")
@@ -155,7 +148,9 @@ def tile_nonlocalmp_pb_t_kernel(tc, h2, F, W3, b3, Wf, b_f, out):
 
         def regroup_w3(engine_copy, block):
             cols = slice(W3_BLOCK * block, W3_BLOCK * (block + 1))
-            regroup(engine_copy, w3_grp[:, cols, :], w3_raw[:, :, cols])
+            rest_cols = slice(W3_BLOCK * (block - 1), W3_BLOCK * block)
+            raw = w3_first[:] if block == 0 else w3_rest[:, :, rest_cols]
+            regroup(engine_copy, w3_grp[:, cols, :], raw)
 
         def quantise_w3(block):
             cols = slice(W3_BLOCK * block, W3_BLOCK * (block + 1))
@@ -177,63 +172,55 @@ def tile_nonlocalmp_pb_t_kernel(tc, h2, F, W3, b3, Wf, b_f, out):
                 stop=stop,
             )
 
-        def relu_sum(r, c, first):
+        def relu_sum(r, c):
             bank = work.tile([P, CHUNK], F32, tag="work")
             message_pass(bank[:], r, c, slice(0, CHUNK), True, True)
-            if through_scalar(r):
-                if first:
+            if through_scalar(r, c):
+                if c == 0:
                     nc.scalar.activation(out=acc[r][:], in_=bank[:], func=ACT.Relu, bias=b3_col[:, r : r + 1])
                 else:
                     relu_sb = hand.tile([P, CHUNK], F32, tag="hand")
                     nc.scalar.activation(out=relu_sb[:], in_=bank[:], func=ACT.Relu, bias=b3_col[:, r : r + 1])
                     nc.gpsimd.tensor_tensor(out=acc[r][:], in0=acc[r][:], in1=relu_sb[:], op=ALU.add)
-            elif first:
+                return
+            dst = mixed_acc if r == MIXED else acc[r]
+            if c == (MIXED_HALF if r == MIXED else 0):
                 nc.vector.tensor_scalar(
-                    out=acc[r][:], in0=bank[:], scalar1=neg_b3[:, r : r + 1], scalar2=None, op0=ALU.max
+                    out=dst[:], in0=bank[:], scalar1=neg_b3[:, r : r + 1], scalar2=None, op0=ALU.max
                 )
             else:
                 nc.vector.scalar_tensor_tensor(
-                    out=acc[r][:],
-                    in0=bank[:],
-                    scalar=neg_b3[:, r : r + 1],
-                    in1=acc[r][:],
-                    op0=ALU.max,
-                    op1=ALU.add,
+                    out=dst[:], in0=bank[:], scalar=neg_b3[:, r : r + 1], in1=dst[:], op0=ALU.max, op1=ALU.add
                 )
 
         plain_sums = {}
 
-        def plain_pass(r, j):
-            if j == 0:
+        def plain_pass(r, j, views=slice(0, VIEWS)):
+            if r not in plain_sums:
                 plain_sums[r] = plain.tile([P, CHUNK], F32, name="plain_sum")
-            jj = j % J_CHUNK
+            start = VIEWS * (j % J_CHUNK)
             message_pass(
-                plain_sums[r][:, 0:VIEWS],
+                plain_sums[r][:, views],
                 r,
                 j // J_CHUNK,
-                slice(VIEWS * jj, VIEWS * (jj + 1)),
+                slice(start + views.start, start + views.stop),
                 j == 0,
                 j == NEIGH - 1,
             )
 
-        def fold(r):
+        def fold(r, dst, src):
             nc.vector.scalar_tensor_tensor(
-                out=folded[:, r, :],
-                in0=acc[r][:, 0:VIEWS],
+                out=dst,
+                in0=src[:, 0:VIEWS],
                 scalar=fold_b3[:, r : r + 1],
-                in1=acc[r][:, VIEWS:CHUNK],
+                in1=src[:, VIEWS:CHUNK],
                 op0=ALU.add,
                 op1=ALU.add,
             )
 
-        def add_plain_sum(r):
+        def add_plain_sum(r, dst):
             nc.vector.scalar_tensor_tensor(
-                out=folded[:, r, :],
-                in0=plain_sums[r][:, 0:VIEWS],
-                scalar=0.25,
-                in1=folded[:, r, :],
-                op0=ALU.mult,
-                op1=ALU.add,
+                out=dst, in0=plain_sums[r][:, 0:VIEWS], scalar=0.25, in1=dst, op0=ALU.mult, op1=ALU.add
             )
 
         def regroup_wf(piece):
@@ -278,80 +265,129 @@ def tile_nonlocalmp_pb_t_kernel(tc, h2, F, W3, b3, Wf, b_f, out):
             )
 
         transpose_chunk(0)
-        nc.vector.tensor_copy(out=b3_rows32[:], in_=b3_rows[:])
+        regroup_w3(nc.vector.tensor_copy, 0)
+        nc.gpsimd.tensor_copy(out=b3_rows32[:], in_=b3_rows[:])
         b3_t = work.tile([P, CHUNK], F32, tag="work")
         nc.tensor.transpose(b3_t[:, 0:P], b3_rows32[:], ident[:])
-        regroup_w3(nc.vector.tensor_copy, 0)
-        regroup_w3(nc.scalar.copy, 1)
-        quantise_chunk(0)
+        transpose_chunk(1)
         quantise_w3(0)
+        quantise_chunk(0)
         nc.vector.tensor_copy(out=b3_col[:], in_=b3_t[:, 0:R_TILES])
         nc.vector.tensor_scalar(out=neg_b3[:], in0=b3_col[:], scalar1=-1.0, scalar2=None, op0=ALU.mult)
-        nc.vector.tensor_scalar(out=fold_b3[:], in0=b3_col[:], scalar1=20.0, scalar2=None, op0=ALU.mult)
-        nc.vector.tensor_scalar(
-            out=fold_b3[:, 1:R_TILES:3], in0=b3_col[:, 1:R_TILES:3], scalar1=4.0, scalar2=None, op0=ALU.mult
-        )
-        regroup_w3(nc.vector.tensor_copy, 2)
-        quantise_w3(1)
-        quantise_w3(2)
+        for r in range(R_TILES):
+            on_vector = [c for c in range(CHUNKS) if not through_scalar(r, c)]
+            factor = 4.0 + J_CHUNK * len(on_vector)
+            nc.gpsimd.tensor_scalar(
+                out=fold_b3[:, r : r + 1], in0=b3_col[:, r : r + 1], scalar1=factor, scalar2=None, op0=ALU.mult
+            )
 
+        tile_a, tile_b = PAIRS[0]
         for c in range(CHUNKS):
-            behind = [(r, J_CHUNK * (c - 1) + jj) for r in late for jj in range(J_CHUNK)] if c > 0 else []
-            for i, r in enumerate(early):
-                relu_sum(r, c, c == 0)
-                for r_plain, j in share(behind, i, len(early)):
-                    plain_pass(r_plain, j)
-                if i == 1 and c == 0:
-                    transpose_chunk(1)
-                if i == 1 and 0 < c < CHUNKS - 1:
-                    quantise_chunk(c + 1)
-            if c == 0:
-                regroup_w3(nc.vector.tensor_copy, 3)
-                quantise_chunk(1)
-                quantise_w3(3)
+            relu_sum(tile_a, c)
+            relu_sum(tile_b, c)
+            if c + 1 < CHUNKS:
+                quantise_chunk(c + 1)
+            for r in (tile_a, tile_b):
+                for jj in range(J_CHUNK):
+                    plain_pass(r, J_CHUNK * c + jj)
             if c + 2 < CHUNKS:
                 transpose_chunk(c + 2)
             if c + 2 == CHUNKS:
                 transpose_pairs(x_grp[:, 0, :, :], f_sb[:].bitcast(F32))
-            if c + 1 == CHUNKS:
-                quantise_x(0, slice(0, VIEWS))
-        for r in late:
-            for jj in range(J_CHUNK):
-                plain_pass(r, NEIGH - J_CHUNK + jj)
-            nc.scalar.activation(out=acc[r][:, 0:VIEWS], in_=plain_sums[r][:, 0:VIEWS], func=ACT.Copy, scale=0.25)
+            if c == CHUNKS - 4:
+                regroup_w3(nc.vector.tensor_copy, 1)
+            if c == CHUNKS - 3:
+                quantise_w3(1)
+        add_plain_sum(tile_a, acc[tile_a][:, 0:VIEWS])
 
-        early_plain = [(r, j) for r in early for j in range(NEIGH)]
+        for pair in (1, 2):
+            tile_a, tile_b = PAIRS[pair]
+            before_a, before_b = PAIRS[pair - 1]
+            units = [(r, j) for r in (tile_a, tile_b) for j in range(NEIGH)]
+            for c in range(CHUNKS):
+                relu_sum(tile_a, c)
+                relu_sum(tile_b, c)
+                for r, j in units[4 * c : 4 * (c + 1)]:
+                    plain_pass(r, j)
+                if c == 0:
+                    fold(before_a, folded[:, before_a, :], acc[before_a])
+                if c == 2:
+                    fold(before_b, folded[:, before_b, :], acc[before_b])
+                    add_plain_sum(before_b, folded[:, before_b, :])
+                if c in (1, 3, 5):
+                    regroup_wf(3 * (pair - 1) + c // 2)
+                if c == 2:
+                    regroup_w3(nc.vector.tensor_copy, pair + 1)
+                if c == 4:
+                    quantise_w3(pair + 1)
+                if c == 5:
+                    add_plain_sum(tile_a, acc[tile_a][:, 0:VIEWS])
+                if pair == 1 and c == 3:
+                    quantise_x(0, slice(0, VIEWS))
+                if pair == 1 and c == 6:
+                    quantise_wf(0)
+                if pair == 2 and c == 3:
+                    regroup_x(1)
+                    quantise_wf(1)
+                if pair == 2 and c == 6:
+                    quantise_x(1, slice(0, VIEWS))
+                    quantise_wf(2)
+
+        before_a, before_b = PAIRS[2]
+        units = [(MIXED, j, slice(0, VIEWS)) for j in range(NEIGH)]
+        for h in range(HALVES):
+            units += [(LAST, j, slice(P * h, P * (h + 1))) for j in range(NEIGH)]
+        columns = 0
         for c in range(CHUNKS):
-            step_plain = early_plain[PLAIN_PER_STEP * c : PLAIN_PER_STEP * (c + 1)]
-            for i, r in enumerate(late):
-                relu_sum(r, c, False)
-                for r_plain, j in share(step_plain, i, len(late)):
-                    plain_pass(r_plain, j)
-            if c < len(early):
-                fold(early[c])
-            for r_plain, j in step_plain:
-                if j == NEIGH - 1:
-                    add_plain_sum(r_plain)
-            if c < 2 * K_PASSES:
-                regroup_wf(c)
-            if c >= 2 and c % 2 == 0:
-                quantise_wf(c // 2 - 1)
+            relu_sum(MIXED, c)
+            relu_sum(LAST, c)
+            while columns < LAST_STEP_COLUMNS * (c + 1):
+                r, j, views = units.pop(0)
+                plain_pass(r, j, views)
+                columns += views.stop - views.start
+            if c == 0:
+                fold(before_a, folded[:, before_a, :], acc[before_a])
+            if c == 2:
+                fold(before_b, folded[:, before_b, :], acc[before_b])
+                add_plain_sum(before_b, folded[:, before_b, :])
+            if c == MIXED_HALF:
+                nc.gpsimd.tensor_tensor(
+                    out=folded[:, MIXED, :], in0=acc[MIXED][:, 0:VIEWS], in1=acc[MIXED][:, VIEWS:CHUNK], op=ALU.add
+                )
+            if c == CHUNKS - 2:
+                add_plain_sum(MIXED, folded[:, MIXED, :])
 
-        for r_plain, j in early_plain[PLAIN_PER_STEP * CHUNKS :]:
-            plain_pass(r_plain, j)
-        regroup_x(1)
-        for r in late:
-            fold(r)
-        quantise_x(1, slice(0, VIEWS))
+        while len(units) > NEIGH:
+            r, j, views = units.pop(0)
+            plain_pass(r, j, views)
         fused = []
         for h in range(HALVES):
             fused.append(work.tile([P, O], F32, tag="work", name="fused"))
             fusion_pass(fused[h], h, 0)
             fusion_pass(fused[h], h, 1)
-        add_plain_sum(early[-1])
+        for r, j, views in units:
+            plain_pass(r, j, views)
+        fold(MIXED, mixed_acc[:, 0:VIEWS], mixed_acc)
+        fold(LAST, folded[:, LAST, :], acc[LAST])
+        nc.vector.tensor_tensor(
+            out=folded[:, MIXED, :], in0=folded[:, MIXED, :], in1=mixed_acc[:, 0:VIEWS], op=ALU.add
+        )
         regroup_x(2)
+        nc.vector.tensor_scalar(
+            out=folded[:, LAST, :], in0=folded[:, LAST, :], scalar1=0.8, scalar2=None, op0=ALU.mult
+        )
         for h in range(HALVES):
-            quantise_x(2, slice(P * h, P * (h + 1)))
+            cols = slice(P * h, P * (h + 1))
+            nc.vector.scalar_tensor_tensor(
+                out=x_grp[:, 2, cols, PACK - 1],
+                in0=plain_sums[LAST][:, cols],
+                scalar=0.2,
+                in1=folded[:, LAST, cols],
+                op0=ALU.mult,
+                op1=ALU.add,
+            )
+            quantise_x(2, cols)
             fusion_pass(fused[h], h, 2)
+        for h in range(HALVES):
             nc.vector.tensor_tensor(out=result[:, h, :], in0=fused[h][:], in1=bf_all[:], op=ALU.add)
             nc.sync.dma_start(out=out_v[:, h, :], in_=result[:, h, :])

@@ -24,13 +24,14 @@ J_CHUNK = NEIGH // CHUNKS
 HALVES = VIEWS // P
 K_PASSES = (D + R) // (P * PACK)
 W3_BLOCK = 256
+W3_LOADS = [1, 1, 2]
 
-PAIRS = [(0, 1), (2, 3), (4, 5), (6, 7)]
+FIRST = 3
+FIRST_PLAIN = 1
 LAST = R_TILES - 1
-MIXED = R_TILES - 2
-VECTOR_START = 2
-MIXED_HALF = CHUNKS // 2
-LAST_STEP_COLUMNS = 5 * P
+SCALAR_CHUNKS = 3
+SLOTS = 8
+PLAIN_AT_END = 8
 
 FLOPS = 2 * VIEWS * NEIGH * Q * R + 2 * VIEWS * (D + R) * O
 
@@ -43,9 +44,11 @@ def regroup(engine_copy, dst, src):
 
 
 def through_scalar(r, c):
-    if r == MIXED:
-        return c < MIXED_HALF
-    return r % 2 == 1 and r != LAST and c >= VECTOR_START
+    return c < (1 if r < FIRST else SCALAR_CHUNKS)
+
+
+def share(items, i, n):
+    return items[len(items) * i // n : len(items) * (i + 1) // n]
 
 
 def tile_nonlocalmp_pb_t_kernel(tc, h2, F, W3, b3, Wf, b_f, out):
@@ -60,8 +63,7 @@ def tile_nonlocalmp_pb_t_kernel(tc, h2, F, W3, b3, Wf, b_f, out):
         name="work", bufs=6
     ) as work, tc.psum_pool(name="plain", bufs=2) as plain, tc.manual_schedule():
         ident = keep.tile([P, P], F32)
-        w3_first = keep.tile([P, PACK, W3_BLOCK], BF16)
-        w3_rest = keep.tile([P, PACK, R - W3_BLOCK], BF16)
+        w3_raw = [keep.tile([P, PACK, n * W3_BLOCK], BF16, name="w3_raw%d" % i) for i, n in enumerate(W3_LOADS)]
         w3_grp = keep.tile([P, R, PACK], BF16, align_bytes=64)
         w3_words = keep.tile([P, R], U32, align_bytes=64)
         w3_scales = keep.tile([P, R], U8, align_bytes=64)
@@ -84,7 +86,6 @@ def tile_nonlocalmp_pb_t_kernel(tc, h2, F, W3, b3, Wf, b_f, out):
         folded = keep.tile([P, R_TILES, VIEWS], F32)
         result = keep.tile([P, HALVES, O], F32)
         acc = [keep.tile([P, CHUNK], F32, name="acc%d" % r) for r in range(R_TILES)]
-        mixed_acc = keep.tile([P, CHUNK], F32)
 
         h2_rows = []
 
@@ -93,20 +94,25 @@ def tile_nonlocalmp_pb_t_kernel(tc, h2, F, W3, b3, Wf, b_f, out):
             nc.sync.dma_start(out=chunk_rows[:], in_=h2_v[:, :, J_CHUNK * c : J_CHUNK * (c + 1), :])
             h2_rows.append(chunk_rows)
 
-        def load_w3(raw, cols):
+        def load_w3(i):
+            first = sum(W3_LOADS[:i])
+            cols = slice(W3_BLOCK * first, W3_BLOCK * (first + W3_LOADS[i]))
             for u in range(2):
                 nc.sync.dma_start(
-                    out=raw[:, 2 * u : 2 * u + 2, :],
+                    out=w3_raw[i][:, 2 * u : 2 * u + 2, :],
                     in_=W3[256 * u : 256 * (u + 1), cols].rearrange("(q e) c -> q e c", e=2),
                 )
 
         nc.vector.memset(b3_rows[:], 0.0)
         nc.scalar.dma_start(out=b3_rows[0:R_TILES, :], in_=b3.rearrange("(r p) -> r p", p=P))
         load_chunk(0)
-        load_w3(w3_first, slice(0, W3_BLOCK))
-        for c in range(1, CHUNKS):
+        load_w3(0)
+        load_chunk(1)
+        load_w3(1)
+        for c in range(2, CHUNKS):
             load_chunk(c)
-        load_w3(w3_rest, slice(W3_BLOCK, R))
+            if c == CHUNKS // 2:
+                load_w3(2)
         nc.sync.dma_start(out=f_sb[:], in_=f_v)
         for u in range(2):
             nc.sync.dma_start(
@@ -148,9 +154,10 @@ def tile_nonlocalmp_pb_t_kernel(tc, h2, F, W3, b3, Wf, b_f, out):
 
         def regroup_w3(engine_copy, block):
             cols = slice(W3_BLOCK * block, W3_BLOCK * (block + 1))
-            rest_cols = slice(W3_BLOCK * (block - 1), W3_BLOCK * block)
-            raw = w3_first[:] if block == 0 else w3_rest[:, :, rest_cols]
-            regroup(engine_copy, w3_grp[:, cols, :], raw)
+            i = min(block, len(W3_LOADS) - 1)
+            first = block - i
+            raw_cols = slice(W3_BLOCK * first, W3_BLOCK * (first + 1))
+            regroup(engine_copy, w3_grp[:, cols, :], w3_raw[i][:, :, raw_cols])
 
         def quantise_w3(block):
             cols = slice(W3_BLOCK * block, W3_BLOCK * (block + 1))
@@ -182,15 +189,14 @@ def tile_nonlocalmp_pb_t_kernel(tc, h2, F, W3, b3, Wf, b_f, out):
                     relu_sb = hand.tile([P, CHUNK], F32, tag="hand")
                     nc.scalar.activation(out=relu_sb[:], in_=bank[:], func=ACT.Relu, bias=b3_col[:, r : r + 1])
                     nc.gpsimd.tensor_tensor(out=acc[r][:], in0=acc[r][:], in1=relu_sb[:], op=ALU.add)
-                return
-            dst = mixed_acc if r == MIXED else acc[r]
-            if c == (MIXED_HALF if r == MIXED else 0):
-                nc.vector.tensor_scalar(
-                    out=dst[:], in0=bank[:], scalar1=neg_b3[:, r : r + 1], scalar2=None, op0=ALU.max
-                )
             else:
                 nc.vector.scalar_tensor_tensor(
-                    out=dst[:], in0=bank[:], scalar=neg_b3[:, r : r + 1], in1=dst[:], op0=ALU.max, op1=ALU.add
+                    out=acc[r][:],
+                    in0=bank[:],
+                    scalar=neg_b3[:, r : r + 1],
+                    in1=acc[r][:],
+                    op0=ALU.max,
+                    op1=ALU.add,
                 )
 
         plain_sums = {}
@@ -208,12 +214,12 @@ def tile_nonlocalmp_pb_t_kernel(tc, h2, F, W3, b3, Wf, b_f, out):
                 j == NEIGH - 1,
             )
 
-        def fold(r, dst, src):
+        def fold(r):
             nc.vector.scalar_tensor_tensor(
-                out=dst,
-                in0=src[:, 0:VIEWS],
+                out=folded[:, r, :],
+                in0=acc[r][:, 0:VIEWS],
                 scalar=fold_b3[:, r : r + 1],
-                in1=src[:, VIEWS:CHUNK],
+                in1=acc[r][:, VIEWS:CHUNK],
                 op0=ALU.add,
                 op1=ALU.add,
             )
@@ -281,97 +287,81 @@ def tile_nonlocalmp_pb_t_kernel(tc, h2, F, W3, b3, Wf, b_f, out):
                 out=fold_b3[:, r : r + 1], in0=b3_col[:, r : r + 1], scalar1=factor, scalar2=None, op0=ALU.mult
             )
 
-        tile_a, tile_b = PAIRS[0]
         for c in range(CHUNKS):
-            relu_sum(tile_a, c)
-            relu_sum(tile_b, c)
-            if c + 1 < CHUNKS:
-                quantise_chunk(c + 1)
-            for r in (tile_a, tile_b):
+            for r in range(FIRST - 1):
+                relu_sum(r, c)
+                if r == 0 and c + 1 < CHUNKS:
+                    quantise_chunk(c + 1)
+            if c > 0:
+                relu_sum(FIRST - 1, c - 1)
+            else:
+                regroup_w3(nc.scalar.copy, 1)
+                quantise_w3(1)
+            for r in range(FIRST_PLAIN):
                 for jj in range(J_CHUNK):
                     plain_pass(r, J_CHUNK * c + jj)
             if c + 2 < CHUNKS:
                 transpose_chunk(c + 2)
             if c + 2 == CHUNKS:
                 transpose_pairs(x_grp[:, 0, :, :], f_sb[:].bitcast(F32))
-            if c == CHUNKS - 4:
-                regroup_w3(nc.vector.tensor_copy, 1)
-            if c == CHUNKS - 3:
-                quantise_w3(1)
-        add_plain_sum(tile_a, acc[tile_a][:, 0:VIEWS])
+            if c in (4, 5):
+                regroup_w3(nc.scalar.copy, c - 2)
+            if c in (6, 7):
+                quantise_w3(c - 4)
+        relu_sum(FIRST - 1, CHUNKS - 1)
+        for c in range(SCALAR_CHUNKS):
+            relu_sum(FIRST, c)
 
-        for pair in (1, 2):
-            tile_a, tile_b = PAIRS[pair]
-            before_a, before_b = PAIRS[pair - 1]
-            units = [(r, j) for r in (tile_a, tile_b) for j in range(NEIGH)]
-            for c in range(CHUNKS):
-                relu_sum(tile_a, c)
-                relu_sum(tile_b, c)
-                for r, j in units[4 * c : 4 * (c + 1)]:
-                    plain_pass(r, j)
-                if c == 0:
-                    fold(before_a, folded[:, before_a, :], acc[before_a])
-                if c == 2:
-                    fold(before_b, folded[:, before_b, :], acc[before_b])
-                    add_plain_sum(before_b, folded[:, before_b, :])
-                if c in (1, 3, 5):
-                    regroup_wf(3 * (pair - 1) + c // 2)
-                if c == 2:
-                    regroup_w3(nc.vector.tensor_copy, pair + 1)
-                if c == 4:
-                    quantise_w3(pair + 1)
-                if c == 5:
-                    add_plain_sum(tile_a, acc[tile_a][:, 0:VIEWS])
-                if pair == 1 and c == 3:
+        passes = [(r, j, slice(0, VIEWS)) for r in range(FIRST_PLAIN, LAST) for j in range(NEIGH)]
+        last_passes = [[(LAST, j, slice(P * h, P * (h + 1))) for j in range(NEIGH)] for h in range(HALVES)]
+        steps = (R_TILES - FIRST) * SLOTS
+        step = 0
+        done = list(range(FIRST_PLAIN))
+        for r in range(FIRST, R_TILES):
+            vector_chunks = list(range(SCALAR_CHUNKS, CHUNKS))
+            scalar_chunks = list(range(SCALAR_CHUNKS)) if r < LAST else []
+            for s in range(SLOTS):
+                for c in share(vector_chunks, s, SLOTS):
+                    relu_sum(r, c)
+                for c in share(scalar_chunks, s, SLOTS):
+                    relu_sum(r + 1, c)
+                ending = done
+                done = []
+                for i, j, views in share(passes[: len(passes) - PLAIN_AT_END], step, steps):
+                    plain_pass(i, j, views)
+                    if j == NEIGH - 1:
+                        done.append(i)
+                if r == FIRST and s < FIRST:
+                    fold(s)
+                if r > FIRST and s == 0:
+                    fold(r - 1)
+                for i in ending:
+                    add_plain_sum(i, folded[:, i, :])
+                step += 1
+                if s in (2, 5) and (r - FIRST) < K_PASSES:
+                    regroup_wf(2 * (r - FIRST) + s // 4)
+                if s == 4 and FIRST < r <= FIRST + K_PASSES:
+                    quantise_wf(r - FIRST - 1)
+                if s == 3 and r == FIRST:
                     quantise_x(0, slice(0, VIEWS))
-                if pair == 1 and c == 6:
-                    quantise_wf(0)
-                if pair == 2 and c == 3:
+                if s == 5 and r == FIRST + 3:
                     regroup_x(1)
-                    quantise_wf(1)
-                if pair == 2 and c == 6:
+                if s == 7 and r == FIRST + 3:
                     quantise_x(1, slice(0, VIEWS))
-                    quantise_wf(2)
 
-        before_a, before_b = PAIRS[2]
-        units = [(MIXED, j, slice(0, VIEWS)) for j in range(NEIGH)]
-        for h in range(HALVES):
-            units += [(LAST, j, slice(P * h, P * (h + 1))) for j in range(NEIGH)]
-        columns = 0
-        for c in range(CHUNKS):
-            relu_sum(MIXED, c)
-            relu_sum(LAST, c)
-            while columns < LAST_STEP_COLUMNS * (c + 1):
-                r, j, views = units.pop(0)
-                plain_pass(r, j, views)
-                columns += views.stop - views.start
-            if c == 0:
-                fold(before_a, folded[:, before_a, :], acc[before_a])
-            if c == 2:
-                fold(before_b, folded[:, before_b, :], acc[before_b])
-                add_plain_sum(before_b, folded[:, before_b, :])
-            if c == MIXED_HALF:
-                nc.gpsimd.tensor_tensor(
-                    out=folded[:, MIXED, :], in0=acc[MIXED][:, 0:VIEWS], in1=acc[MIXED][:, VIEWS:CHUNK], op=ALU.add
-                )
-            if c == CHUNKS - 2:
-                add_plain_sum(MIXED, folded[:, MIXED, :])
-
-        while len(units) > NEIGH:
-            r, j, views = units.pop(0)
-            plain_pass(r, j, views)
+        for i in done:
+            add_plain_sum(i, folded[:, i, :])
+        fold(LAST)
+        for i, j, views in passes[len(passes) - PLAIN_AT_END :] + last_passes[0]:
+            plain_pass(i, j, views)
         fused = []
         for h in range(HALVES):
             fused.append(work.tile([P, O], F32, tag="work", name="fused"))
             fusion_pass(fused[h], h, 0)
             fusion_pass(fused[h], h, 1)
-        for r, j, views in units:
-            plain_pass(r, j, views)
-        fold(MIXED, mixed_acc[:, 0:VIEWS], mixed_acc)
-        fold(LAST, folded[:, LAST, :], acc[LAST])
-        nc.vector.tensor_tensor(
-            out=folded[:, MIXED, :], in0=folded[:, MIXED, :], in1=mixed_acc[:, 0:VIEWS], op=ALU.add
-        )
+        for i, j, views in last_passes[1]:
+            plain_pass(i, j, views)
+        add_plain_sum(LAST - 1, folded[:, LAST - 1, :])
         regroup_x(2)
         nc.vector.tensor_scalar(
             out=folded[:, LAST, :], in0=folded[:, LAST, :], scalar1=0.8, scalar2=None, op0=ALU.mult

@@ -26,11 +26,12 @@ K_PASSES = (D + R) // (P * PACK)
 W3_BLOCK = 256
 W3_LOADS = [1, 1, 2]
 
-FIRST = 3
-FIRST_PLAIN = 1
-LAST = R_TILES - 1
-SCALAR_CHUNKS = 3
-SLOTS = 8
+HEAD = (0, 1)
+THIRD = 2
+GROUPS = ((3, 4), (5, 7, 6))
+ON_SCALAR = (4, 7)
+PLAIN_ORDER = (1, 2, 3, 5, 4, 7, 6)
+LAST = PLAIN_ORDER[-1]
 PLAIN_AT_END = 8
 
 FLOPS = 2 * VIEWS * NEIGH * Q * R + 2 * VIEWS * (D + R) * O
@@ -44,7 +45,7 @@ def regroup(engine_copy, dst, src):
 
 
 def through_scalar(r, c):
-    return c < (1 if r < FIRST else SCALAR_CHUNKS)
+    return r in ON_SCALAR or (c == 0 and r <= THIRD)
 
 
 def share(items, i, n):
@@ -189,6 +190,10 @@ def tile_nonlocalmp_pb_t_kernel(tc, h2, F, W3, b3, Wf, b_f, out):
                     relu_sb = hand.tile([P, CHUNK], F32, tag="hand")
                     nc.scalar.activation(out=relu_sb[:], in_=bank[:], func=ACT.Relu, bias=b3_col[:, r : r + 1])
                     nc.gpsimd.tensor_tensor(out=acc[r][:], in0=acc[r][:], in1=relu_sb[:], op=ALU.add)
+            elif c == 0:
+                nc.vector.tensor_scalar(
+                    out=acc[r][:], in0=bank[:], scalar1=neg_b3[:, r : r + 1], scalar2=None, op0=ALU.max
+                )
             else:
                 nc.vector.scalar_tensor_tensor(
                     out=acc[r][:],
@@ -288,18 +293,17 @@ def tile_nonlocalmp_pb_t_kernel(tc, h2, F, W3, b3, Wf, b_f, out):
             )
 
         for c in range(CHUNKS):
-            for r in range(FIRST - 1):
+            for r in HEAD:
                 relu_sum(r, c)
                 if r == 0 and c + 1 < CHUNKS:
                     quantise_chunk(c + 1)
-            if c > 0:
-                relu_sum(FIRST - 1, c - 1)
-            else:
+            if c % 2 == 1:
+                relu_sum(THIRD, c - 1)
+            if c == 0:
                 regroup_w3(nc.scalar.copy, 1)
                 quantise_w3(1)
-            for r in range(FIRST_PLAIN):
-                for jj in range(J_CHUNK):
-                    plain_pass(r, J_CHUNK * c + jj)
+            for jj in range(J_CHUNK):
+                plain_pass(0, J_CHUNK * c + jj)
             if c + 2 < CHUNKS:
                 transpose_chunk(c + 2)
             if c + 2 == CHUNKS:
@@ -308,60 +312,69 @@ def tile_nonlocalmp_pb_t_kernel(tc, h2, F, W3, b3, Wf, b_f, out):
                 regroup_w3(nc.scalar.copy, c - 2)
             if c in (6, 7):
                 quantise_w3(c - 4)
-        relu_sum(FIRST - 1, CHUNKS - 1)
-        for c in range(SCALAR_CHUNKS):
-            relu_sum(FIRST, c)
 
-        passes = [(r, j, slice(0, VIEWS)) for r in range(FIRST_PLAIN, LAST) for j in range(NEIGH)]
+        order = []
+        for c in range(CHUNKS):
+            order += [(r, c) for r in GROUPS[0]]
+            if c < CHUNKS // 2:
+                order.append((THIRD, 2 * c + 1))
+        order += [(r, c) for c in range(CHUNKS) for r in GROUPS[1]]
+        passes = [(r, j, slice(0, VIEWS)) for r in PLAIN_ORDER[:-1] for j in range(NEIGH)]
         last_passes = [[(LAST, j, slice(P * h, P * (h + 1))) for j in range(NEIGH)] for h in range(HALVES)]
-        steps = (R_TILES - FIRST) * SLOTS
-        step = 0
-        done = list(range(FIRST_PLAIN))
-        for r in range(FIRST, R_TILES):
-            vector_chunks = list(range(SCALAR_CHUNKS, CHUNKS))
-            scalar_chunks = list(range(SCALAR_CHUNKS)) if r < LAST else []
-            for s in range(SLOTS):
-                for c in share(vector_chunks, s, SLOTS):
-                    relu_sum(r, c)
-                for c in share(scalar_chunks, s, SLOTS):
-                    relu_sum(r + 1, c)
-                ending = done
-                done = []
-                for i, j, views in share(passes[: len(passes) - PLAIN_AT_END], step, steps):
-                    plain_pass(i, j, views)
-                    if j == NEIGH - 1:
-                        done.append(i)
-                if r == FIRST and s < FIRST:
-                    fold(s)
-                if r > FIRST and s == 0:
-                    fold(r - 1)
-                for i in ending:
-                    add_plain_sum(i, folded[:, i, :])
-                step += 1
-                if s in (2, 5) and (r - FIRST) < K_PASSES:
-                    regroup_wf(2 * (r - FIRST) + s // 4)
-                if s == 4 and FIRST < r <= FIRST + K_PASSES:
-                    quantise_wf(r - FIRST - 1)
-                if s == 3 and r == FIRST:
-                    quantise_x(0, slice(0, VIEWS))
-                if s == 5 and r == FIRST + 3:
-                    regroup_x(1)
-                if s == 7 and r == FIRST + 3:
-                    quantise_x(1, slice(0, VIEWS))
+        along = len(passes) - PLAIN_AT_END
+        closed = [0]
+        for i, (r, c) in enumerate(order):
+            relu_sum(r, c)
+            ready = closed
+            closed = []
+            for r_plain, j, views in share(passes[:along], i, len(order)):
+                plain_pass(r_plain, j, views)
+                if j == NEIGH - 1:
+                    closed.append(r_plain)
+            for r_plain in ready:
+                if r_plain in ON_SCALAR:
+                    add_plain_sum(r_plain, folded[:, r_plain, :])
+                else:
+                    add_plain_sum(r_plain, acc[r_plain][:, 0:VIEWS])
+            if (r, c) == (3, 1):
+                fold(0)
+            if (r, c) == (3, 3):
+                quantise_x(0, slice(0, VIEWS))
+            if (r, c) == (3, 4):
+                fold(1)
+            if (r, c) == (5, 0):
+                fold(2)
+            if (r, c) == (5, 2):
+                fold(3)
+            if (r, c) == (7, 2):
+                fold(4)
+            if r == 4 and c in (1, 4, 7):
+                regroup_wf(c // 3)
+            if r == 7 and c in (1, 3, 5):
+                regroup_wf(3 + c // 2)
+            if (r, c) == (3, 7):
+                quantise_wf(0)
+            if (r, c) == (6, 3):
+                regroup_x(1)
+                quantise_wf(1)
+            if (r, c) == (6, 4):
+                quantise_x(1, slice(0, VIEWS))
+            if (r, c) == (6, 6):
+                quantise_wf(2)
 
-        for i in done:
-            add_plain_sum(i, folded[:, i, :])
+        fold(5)
         fold(LAST)
-        for i, j, views in passes[len(passes) - PLAIN_AT_END :] + last_passes[0]:
-            plain_pass(i, j, views)
+        for r_plain, j, views in passes[along:] + last_passes[0]:
+            plain_pass(r_plain, j, views)
         fused = []
         for h in range(HALVES):
             fused.append(work.tile([P, O], F32, tag="work", name="fused"))
             fusion_pass(fused[h], h, 0)
             fusion_pass(fused[h], h, 1)
-        for i, j, views in last_passes[1]:
-            plain_pass(i, j, views)
-        add_plain_sum(LAST - 1, folded[:, LAST - 1, :])
+        for r_plain, j, views in last_passes[1]:
+            plain_pass(r_plain, j, views)
+        fold(7)
+        add_plain_sum(7, folded[:, 7, :])
         regroup_x(2)
         nc.vector.tensor_scalar(
             out=folded[:, LAST, :], in0=folded[:, LAST, :], scalar1=0.8, scalar2=None, op0=ALU.mult
@@ -369,7 +382,7 @@ def tile_nonlocalmp_pb_t_kernel(tc, h2, F, W3, b3, Wf, b_f, out):
         for h in range(HALVES):
             cols = slice(P * h, P * (h + 1))
             nc.vector.scalar_tensor_tensor(
-                out=x_grp[:, 2, cols, PACK - 1],
+                out=x_grp[:, 2, cols, LAST % PACK],
                 in0=plain_sums[LAST][:, cols],
                 scalar=0.2,
                 in1=folded[:, LAST, cols],

@@ -27,10 +27,11 @@ W3_BLOCK = 256
 W3_LOADS = [1, 1, 2]
 
 HEAD = (0, 1)
-THIRD = 2
-GROUPS = ((3, 4), (5, 7, 6))
+GROUPS = ((2, 4, 3), (5, 7, 6))
 ON_SCALAR = (4, 7)
-PLAIN_ORDER = (1, 2, 3, 5, 4, 7, 6)
+ON_GPSIMD = (0, 1, 2, 3, 7)
+PLAIN_FIRST = 5
+PLAIN_ORDER = (5, 1, 2, 3, 6, 7, 4)
 LAST = PLAIN_ORDER[-1]
 PLAIN_AT_END = 8
 
@@ -45,7 +46,7 @@ def regroup(engine_copy, dst, src):
 
 
 def through_scalar(r, c):
-    return r in ON_SCALAR or (c == 0 and r <= THIRD)
+    return r in ON_SCALAR or (c == 0 and r in HEAD)
 
 
 def share(items, i, n):
@@ -85,6 +86,7 @@ def tile_nonlocalmp_pb_t_kernel(tc, h2, F, W3, b3, Wf, b_f, out):
         fold_b3 = keep.tile([P, R_TILES], F32)
         bf_all = keep.tile([P, O], BF16)
         folded = keep.tile([P, R_TILES, VIEWS], F32)
+        last_sum = keep.tile([P, VIEWS], F32)
         result = keep.tile([P, HALVES, O], F32)
         acc = [keep.tile([P, CHUNK], F32, name="acc%d" % r) for r in range(R_TILES)]
 
@@ -128,6 +130,7 @@ def tile_nonlocalmp_pb_t_kernel(tc, h2, F, W3, b3, Wf, b_f, out):
         nc.sync.dma_start(out=bf_all[:], in_=b_f.partition_broadcast(P))
 
         make_identity(nc, ident[:])
+        nc.gpsimd.memset(acc[PLAIN_FIRST][:, VIEWS:CHUNK], 0.0)
 
         def transpose_pairs(dst_grp, src_words):
             xt = work.tile([P, 2, HALVES * P], F32, tag="work")
@@ -153,12 +156,11 @@ def tile_nonlocalmp_pb_t_kernel(tc, h2, F, W3, b3, Wf, b_f, out):
                 in_=chunk_grps[c][:].rearrange("p c t -> p (c t)"),
             )
 
-        def regroup_w3(engine_copy, block):
-            cols = slice(W3_BLOCK * block, W3_BLOCK * (block + 1))
-            i = min(block, len(W3_LOADS) - 1)
-            first = block - i
-            raw_cols = slice(W3_BLOCK * first, W3_BLOCK * (first + 1))
-            regroup(engine_copy, w3_grp[:, cols, :], w3_raw[i][:, :, raw_cols])
+        def regroup_w3(engine_copy, r, tiles=1):
+            i = min(P * r // W3_BLOCK, len(W3_LOADS) - 1)
+            first = P * r - W3_BLOCK * i
+            raw_cols = slice(first, first + P * tiles)
+            regroup(engine_copy, w3_grp[:, P * r : P * (r + tiles), :], w3_raw[i][:, :, raw_cols])
 
         def quantise_w3(block):
             cols = slice(W3_BLOCK * block, W3_BLOCK * (block + 1))
@@ -190,7 +192,7 @@ def tile_nonlocalmp_pb_t_kernel(tc, h2, F, W3, b3, Wf, b_f, out):
                     relu_sb = hand.tile([P, CHUNK], F32, tag="hand")
                     nc.scalar.activation(out=relu_sb[:], in_=bank[:], func=ACT.Relu, bias=b3_col[:, r : r + 1])
                     nc.gpsimd.tensor_tensor(out=acc[r][:], in0=acc[r][:], in1=relu_sb[:], op=ALU.add)
-            elif c == 0:
+            elif c == 0 and r != PLAIN_FIRST:
                 nc.vector.tensor_scalar(
                     out=acc[r][:], in0=bank[:], scalar1=neg_b3[:, r : r + 1], scalar2=None, op0=ALU.max
                 )
@@ -234,9 +236,23 @@ def tile_nonlocalmp_pb_t_kernel(tc, h2, F, W3, b3, Wf, b_f, out):
                 out=dst, in0=plain_sums[r][:, 0:VIEWS], scalar=0.25, in1=dst, op0=ALU.mult, op1=ALU.add
             )
 
+        def finish(r):
+            plain_sb = hand.tile([P, VIEWS], F32, tag="plain_sb")
+            nc.scalar.activation(
+                out=plain_sb[:],
+                in_=plain_sums[r][:, 0:VIEWS],
+                func=ACT.Identity,
+                scale=0.25,
+                bias=fold_b3[:, r : r + 1],
+            )
+            nc.gpsimd.tensor_tensor(
+                out=folded[:, r, :], in0=acc[r][:, 0:VIEWS], in1=acc[r][:, VIEWS:CHUNK], op=ALU.add
+            )
+            nc.gpsimd.tensor_tensor(out=folded[:, r, :], in0=folded[:, r, :], in1=plain_sb[:], op=ALU.add)
+
         def regroup_wf(piece):
-            g = piece // 2
-            cols = slice((O // 2) * (piece % 2), (O // 2) * (piece % 2 + 1))
+            g = piece // 4
+            cols = slice((O // 4) * (piece % 4), (O // 4) * (piece % 4 + 1))
             regroup(nc.scalar.copy, wf_grp[:, g, cols, :], wf_raw[:, g, :, cols])
 
         def quantise_wf(g):
@@ -276,7 +292,7 @@ def tile_nonlocalmp_pb_t_kernel(tc, h2, F, W3, b3, Wf, b_f, out):
             )
 
         transpose_chunk(0)
-        regroup_w3(nc.vector.tensor_copy, 0)
+        regroup_w3(nc.vector.tensor_copy, 0, 2)
         nc.gpsimd.tensor_copy(out=b3_rows32[:], in_=b3_rows[:])
         b3_t = work.tile([P, CHUNK], F32, tag="work")
         nc.tensor.transpose(b3_t[:, 0:P], b3_rows32[:], ident[:])
@@ -288,6 +304,8 @@ def tile_nonlocalmp_pb_t_kernel(tc, h2, F, W3, b3, Wf, b_f, out):
         for r in range(R_TILES):
             on_vector = [c for c in range(CHUNKS) if not through_scalar(r, c)]
             factor = 4.0 + J_CHUNK * len(on_vector)
+            if r == LAST:
+                factor = 0.8 * factor
             nc.gpsimd.tensor_scalar(
                 out=fold_b3[:, r : r + 1], in0=b3_col[:, r : r + 1], scalar1=factor, scalar2=None, op0=ALU.mult
             )
@@ -297,10 +315,8 @@ def tile_nonlocalmp_pb_t_kernel(tc, h2, F, W3, b3, Wf, b_f, out):
                 relu_sum(r, c)
                 if r == 0 and c + 1 < CHUNKS:
                     quantise_chunk(c + 1)
-            if c % 2 == 1:
-                relu_sum(THIRD, c - 1)
             if c == 0:
-                regroup_w3(nc.scalar.copy, 1)
+                regroup_w3(nc.scalar.copy, 2, 2)
                 quantise_w3(1)
             for jj in range(J_CHUNK):
                 plain_pass(0, J_CHUNK * c + jj)
@@ -308,17 +324,14 @@ def tile_nonlocalmp_pb_t_kernel(tc, h2, F, W3, b3, Wf, b_f, out):
                 transpose_chunk(c + 2)
             if c + 2 == CHUNKS:
                 transpose_pairs(x_grp[:, 0, :, :], f_sb[:].bitcast(F32))
-            if c in (4, 5):
-                regroup_w3(nc.scalar.copy, c - 2)
+            if c in (2, 3, 4, 5):
+                regroup_w3(nc.scalar.copy, c + 2)
             if c in (6, 7):
-                quantise_w3(c - 4)
+                regroup_wf(c - 6)
+            if c in (4, 6):
+                quantise_w3(c // 2)
 
-        order = []
-        for c in range(CHUNKS):
-            order += [(r, c) for r in GROUPS[0]]
-            if c < CHUNKS // 2:
-                order.append((THIRD, 2 * c + 1))
-        order += [(r, c) for c in range(CHUNKS) for r in GROUPS[1]]
+        order = [(r, c) for group in GROUPS for c in range(CHUNKS) for r in group]
         passes = [(r, j, slice(0, VIEWS)) for r in PLAIN_ORDER[:-1] for j in range(NEIGH)]
         last_passes = [[(LAST, j, slice(P * h, P * (h + 1))) for j in range(NEIGH)] for h in range(HALVES)]
         along = len(passes) - PLAIN_AT_END
@@ -332,39 +345,45 @@ def tile_nonlocalmp_pb_t_kernel(tc, h2, F, W3, b3, Wf, b_f, out):
                 if j == NEIGH - 1:
                     closed.append(r_plain)
             for r_plain in ready:
-                if r_plain in ON_SCALAR:
-                    add_plain_sum(r_plain, folded[:, r_plain, :])
+                if r_plain in ON_GPSIMD:
+                    finish(r_plain)
+                elif r_plain == PLAIN_FIRST:
+                    nc.scalar.activation(
+                        out=acc[r_plain][:, 0:VIEWS],
+                        in_=plain_sums[r_plain][:, 0:VIEWS],
+                        func=ACT.Copy,
+                        scale=0.25,
+                    )
                 else:
                     add_plain_sum(r_plain, acc[r_plain][:, 0:VIEWS])
-            if (r, c) == (3, 1):
-                fold(0)
             if (r, c) == (3, 3):
                 quantise_x(0, slice(0, VIEWS))
-            if (r, c) == (3, 4):
-                fold(1)
-            if (r, c) == (5, 0):
-                fold(2)
-            if (r, c) == (5, 2):
-                fold(3)
+            if r == 4:
+                regroup_wf(2 + c)
+            if r == 7 and c in (0, 1):
+                regroup_wf(10 + c)
             if (r, c) == (7, 2):
-                fold(4)
-            if r == 4 and c in (1, 4, 7):
-                regroup_wf(c // 3)
-            if r == 7 and c in (1, 3, 5):
-                regroup_wf(3 + c // 2)
-            if (r, c) == (3, 7):
-                quantise_wf(0)
-            if (r, c) == (6, 3):
-                regroup_x(1)
-                quantise_wf(1)
-            if (r, c) == (6, 4):
-                quantise_x(1, slice(0, VIEWS))
-            if (r, c) == (6, 6):
+                nc.gpsimd.tensor_tensor(
+                    out=folded[:, LAST, :], in0=acc[LAST][:, 0:VIEWS], in1=acc[LAST][:, VIEWS:CHUNK], op=ALU.add
+                )
+                nc.scalar.activation(
+                    out=last_sum[:], in_=folded[:, LAST, :], func=ACT.Identity, scale=0.8, bias=fold_b3[:, LAST : LAST + 1]
+                )
+            if (r, c) in ((3, 3), (3, 7)):
+                quantise_wf(c // 4)
+            if (r, c) == (5, 3):
                 quantise_wf(2)
+            if (r, c) == (6, 5):
+                regroup_x(1)
+            if (r, c) == (6, 6):
+                quantise_x(1, slice(0, VIEWS))
 
         fold(5)
-        fold(LAST)
-        for r_plain, j, views in passes[along:] + last_passes[0]:
+        fold(6)
+        for r_plain, j, views in passes[along:]:
+            plain_pass(r_plain, j, views)
+        finish(7)
+        for r_plain, j, views in last_passes[0]:
             plain_pass(r_plain, j, views)
         fused = []
         for h in range(HALVES):
@@ -373,19 +392,14 @@ def tile_nonlocalmp_pb_t_kernel(tc, h2, F, W3, b3, Wf, b_f, out):
             fusion_pass(fused[h], h, 1)
         for r_plain, j, views in last_passes[1]:
             plain_pass(r_plain, j, views)
-        fold(7)
-        add_plain_sum(7, folded[:, 7, :])
         regroup_x(2)
-        nc.vector.tensor_scalar(
-            out=folded[:, LAST, :], in0=folded[:, LAST, :], scalar1=0.8, scalar2=None, op0=ALU.mult
-        )
         for h in range(HALVES):
             cols = slice(P * h, P * (h + 1))
             nc.vector.scalar_tensor_tensor(
                 out=x_grp[:, 2, cols, LAST % PACK],
                 in0=plain_sums[LAST][:, cols],
                 scalar=0.2,
-                in1=folded[:, LAST, cols],
+                in1=last_sum[:, cols],
                 op0=ALU.mult,
                 op1=ALU.add,
             )

@@ -29,11 +29,12 @@ W3_LOADS = [1, 1, 2]
 HEAD = (0, 1)
 GROUPS = ((2, 4, 3), (5, 7, 6))
 ON_SCALAR = (4, 7)
-ON_GPSIMD = (0, 1, 2, 3, 7)
 PLAIN_FIRST = 5
-PLAIN_ORDER = (5, 1, 2, 3, 6, 7, 4)
+PLAIN_ORDER = (5, 2, 3, 6, 7, 4)
 LAST = PLAIN_ORDER[-1]
 PLAIN_AT_END = 8
+
+B3_FACTORS = [(0, 4, 18.0), (4, 5, 4.8), (5, 6, 20.0), (6, 7, 18.0), (7, 8, 6.0)]
 
 FLOPS = 2 * VIEWS * NEIGH * Q * R + 2 * VIEWS * (D + R) * O
 
@@ -46,7 +47,7 @@ def regroup(engine_copy, dst, src):
 
 
 def through_scalar(r, c):
-    return r in ON_SCALAR or (c == 0 and r in HEAD)
+    return c == 0 and r != PLAIN_FIRST or c > 1 and r in ON_SCALAR
 
 
 def share(items, i, n):
@@ -107,8 +108,8 @@ def tile_nonlocalmp_pb_t_kernel(tc, h2, F, W3, b3, Wf, b_f, out):
                 )
 
         nc.vector.memset(b3_rows[:], 0.0)
-        nc.scalar.dma_start(out=b3_rows[0:R_TILES, :], in_=b3.rearrange("(r p) -> r p", p=P))
         load_chunk(0)
+        nc.sync.dma_start(out=b3_rows[0:R_TILES, :], in_=b3.rearrange("(r p) -> r p", p=P))
         load_w3(0)
         load_chunk(1)
         load_w3(1)
@@ -156,7 +157,7 @@ def tile_nonlocalmp_pb_t_kernel(tc, h2, F, W3, b3, Wf, b_f, out):
                 in_=chunk_grps[c][:].rearrange("p c t -> p (c t)"),
             )
 
-        def regroup_w3(engine_copy, r, tiles=1):
+        def regroup_w3(engine_copy, r, tiles):
             i = min(P * r // W3_BLOCK, len(W3_LOADS) - 1)
             first = P * r - W3_BLOCK * i
             raw_cols = slice(first, first + P * tiles)
@@ -192,10 +193,6 @@ def tile_nonlocalmp_pb_t_kernel(tc, h2, F, W3, b3, Wf, b_f, out):
                     relu_sb = hand.tile([P, CHUNK], F32, tag="hand")
                     nc.scalar.activation(out=relu_sb[:], in_=bank[:], func=ACT.Relu, bias=b3_col[:, r : r + 1])
                     nc.gpsimd.tensor_tensor(out=acc[r][:], in0=acc[r][:], in1=relu_sb[:], op=ALU.add)
-            elif c == 0 and r != PLAIN_FIRST:
-                nc.vector.tensor_scalar(
-                    out=acc[r][:], in0=bank[:], scalar1=neg_b3[:, r : r + 1], scalar2=None, op0=ALU.max
-                )
             else:
                 nc.vector.scalar_tensor_tensor(
                     out=acc[r][:],
@@ -208,7 +205,7 @@ def tile_nonlocalmp_pb_t_kernel(tc, h2, F, W3, b3, Wf, b_f, out):
 
         plain_sums = {}
 
-        def plain_pass(r, j, views=slice(0, VIEWS)):
+        def plain_pass(r, j, views):
             if r not in plain_sums:
                 plain_sums[r] = plain.tile([P, CHUNK], F32, name="plain_sum")
             start = VIEWS * (j % J_CHUNK)
@@ -292,62 +289,51 @@ def tile_nonlocalmp_pb_t_kernel(tc, h2, F, W3, b3, Wf, b_f, out):
             )
 
         transpose_chunk(0)
+        transpose_chunk(1)
         regroup_w3(nc.vector.tensor_copy, 0, 2)
         nc.gpsimd.tensor_copy(out=b3_rows32[:], in_=b3_rows[:])
         b3_t = work.tile([P, CHUNK], F32, tag="work")
         nc.tensor.transpose(b3_t[:, 0:P], b3_rows32[:], ident[:])
-        transpose_chunk(1)
         quantise_w3(0)
         quantise_chunk(0)
         nc.vector.tensor_copy(out=b3_col[:], in_=b3_t[:, 0:R_TILES])
         nc.vector.tensor_scalar(out=neg_b3[:], in0=b3_col[:], scalar1=-1.0, scalar2=None, op0=ALU.mult)
-        for r in range(R_TILES):
-            on_vector = [c for c in range(CHUNKS) if not through_scalar(r, c)]
-            factor = 4.0 + J_CHUNK * len(on_vector)
-            if r == LAST:
-                factor = 0.8 * factor
-            nc.gpsimd.tensor_scalar(
-                out=fold_b3[:, r : r + 1], in0=b3_col[:, r : r + 1], scalar1=factor, scalar2=None, op0=ALU.mult
-            )
-
         for c in range(CHUNKS):
             for r in HEAD:
                 relu_sum(r, c)
                 if r == 0 and c + 1 < CHUNKS:
                     quantise_chunk(c + 1)
-            if c == 0:
-                regroup_w3(nc.scalar.copy, 2, 2)
-                quantise_w3(1)
-            for jj in range(J_CHUNK):
-                plain_pass(0, J_CHUNK * c + jj)
+            for r in HEAD:
+                for jj in range(J_CHUNK):
+                    plain_pass(r, J_CHUNK * c + jj, slice(0, VIEWS))
             if c + 2 < CHUNKS:
                 transpose_chunk(c + 2)
             if c + 2 == CHUNKS:
                 transpose_pairs(x_grp[:, 0, :, :], f_sb[:].bitcast(F32))
-            if c in (2, 3, 4, 5):
-                regroup_w3(nc.scalar.copy, c + 2)
-            if c in (6, 7):
-                regroup_wf(c - 6)
+            if 1 <= c <= 6:
+                regroup_w3(nc.scalar.copy, c + 1, 1)
             if c in (4, 6):
-                quantise_w3(c // 2)
+                quantise_w3(c // 2 - 1)
+            if c == 1:
+                for first, last, factor in B3_FACTORS:
+                    nc.scalar.activation(
+                        out=fold_b3[:, first:last], in_=b3_col[:, first:last], func=ACT.Copy, scale=factor
+                    )
+
+        for r in HEAD:
+            finish(r)
 
         order = [(r, c) for group in GROUPS for c in range(CHUNKS) for r in group]
         passes = [(r, j, slice(0, VIEWS)) for r in PLAIN_ORDER[:-1] for j in range(NEIGH)]
         last_passes = [[(LAST, j, slice(P * h, P * (h + 1))) for j in range(NEIGH)] for h in range(HALVES)]
         along = len(passes) - PLAIN_AT_END
-        closed = [0]
+        closed = []
         for i, (r, c) in enumerate(order):
             relu_sum(r, c)
             ready = closed
             closed = []
-            for r_plain, j, views in share(passes[:along], i, len(order)):
-                plain_pass(r_plain, j, views)
-                if j == NEIGH - 1:
-                    closed.append(r_plain)
             for r_plain in ready:
-                if r_plain in ON_GPSIMD:
-                    finish(r_plain)
-                elif r_plain == PLAIN_FIRST:
+                if r_plain == PLAIN_FIRST:
                     nc.scalar.activation(
                         out=acc[r_plain][:, 0:VIEWS],
                         in_=plain_sums[r_plain][:, 0:VIEWS],
@@ -356,23 +342,32 @@ def tile_nonlocalmp_pb_t_kernel(tc, h2, F, W3, b3, Wf, b_f, out):
                     )
                 else:
                     add_plain_sum(r_plain, acc[r_plain][:, 0:VIEWS])
+            for r_plain, j, views in share(passes[:along], i, len(order)):
+                plain_pass(r_plain, j, views)
+                if j == NEIGH - 1:
+                    closed.append(r_plain)
             if (r, c) == (3, 3):
                 quantise_x(0, slice(0, VIEWS))
             if r == 4:
-                regroup_wf(2 + c)
-            if r == 7 and c in (0, 1):
-                regroup_wf(10 + c)
-            if (r, c) == (7, 2):
+                regroup_wf(c)
+            if r == 7 and c < 4:
+                regroup_wf(8 + c)
+            if (r, c) == (7, 1):
                 nc.gpsimd.tensor_tensor(
                     out=folded[:, LAST, :], in0=acc[LAST][:, 0:VIEWS], in1=acc[LAST][:, VIEWS:CHUNK], op=ALU.add
                 )
-                nc.scalar.activation(
-                    out=last_sum[:], in_=folded[:, LAST, :], func=ACT.Identity, scale=0.8, bias=fold_b3[:, LAST : LAST + 1]
-                )
-            if (r, c) in ((3, 3), (3, 7)):
-                quantise_wf(c // 4)
-            if (r, c) == (5, 3):
+            if (r, c) == (3, 4):
+                quantise_wf(0)
+            if (r, c) == (5, 1):
+                quantise_wf(1)
+            if (r, c) == (5, 5):
                 quantise_wf(2)
+            if (r, c) == (5, 2):
+                fold(2)
+            if (r, c) == (5, 4):
+                fold(3)
+            if (r, c) == (3, 5):
+                quantise_w3(3)
             if (r, c) == (6, 5):
                 regroup_x(1)
             if (r, c) == (6, 6):
@@ -382,6 +377,9 @@ def tile_nonlocalmp_pb_t_kernel(tc, h2, F, W3, b3, Wf, b_f, out):
         fold(6)
         for r_plain, j, views in passes[along:]:
             plain_pass(r_plain, j, views)
+        nc.scalar.activation(
+            out=last_sum[:], in_=folded[:, LAST, :], func=ACT.Identity, scale=0.8, bias=fold_b3[:, LAST : LAST + 1]
+        )
         finish(7)
         for r_plain, j, views in last_passes[0]:
             plain_pass(r_plain, j, views)

@@ -36,6 +36,8 @@ PLAIN_AT_END = 8
 
 B3_FACTORS = [(0, 4, 18.0), (4, 5, 4.8), (5, 6, 20.0), (6, 7, 18.0), (7, 8, 6.0)]
 
+WARM_UP = 6
+
 FLOPS = 2 * VIEWS * NEIGH * Q * R + 2 * VIEWS * (D + R) * O
 
 
@@ -80,6 +82,7 @@ def tile_nonlocalmp_pb_t_kernel(tc, h2, F, W3, b3, Wf, b_f, out):
         x_words = keep.tile([P, K_PASSES, VIEWS], U32, align_bytes=64)
         x_scales = keep.tile([P, K_PASSES, VIEWS], U8, align_bytes=64)
         f_sb = keep.tile([P, HALVES, D], BF16)
+        zeros = keep.tile([P, CHUNK], BF16)
         b3_rows = keep.tile([P, P], BF16)
         b3_rows32 = keep.tile([P, P], F32)
         b3_col = keep.tile([P, R_TILES], F32)
@@ -107,6 +110,7 @@ def tile_nonlocalmp_pb_t_kernel(tc, h2, F, W3, b3, Wf, b_f, out):
                     in_=W3[256 * u : 256 * (u + 1), cols].rearrange("(q e) c -> q e c", e=2),
                 )
 
+        nc.vector.memset(zeros[:], 0.0)
         nc.vector.memset(b3_rows[:], 0.0)
         load_chunk(0)
         nc.sync.dma_start(out=b3_rows[0:R_TILES, :], in_=b3.rearrange("(r p) -> r p", p=P))
@@ -288,6 +292,9 @@ def tile_nonlocalmp_pb_t_kernel(tc, h2, F, W3, b3, Wf, b_f, out):
                 stop=(g == K_PASSES - 1),
             )
 
+        for i in range(WARM_UP):
+            idle_bank = work.tile([P, CHUNK], F32, tag="work")
+            nc.tensor.matmul(out=idle_bank[:], lhsT=zeros[:, 0:P], rhs=zeros[:], start=True, stop=True)
         transpose_chunk(0)
         transpose_chunk(1)
         regroup_w3(nc.vector.tensor_copy, 0, 2)

import concourse.mybir as mybir
from concourse.masks import make_identity

F32 = mybir.dt.float32
BF16 = mybir.dt.bfloat16
U32 = mybir.dt.uint32
U8 = mybir.dt.uint8
FP8X4 = mybir.dt.float8_e4m3fn_x4
ALU = mybir.AluOpType
ACT = mybir.ActivationFunctionType

P = 128
PACK = 4
VIEWS = 256
NEIGH = 16
Q = 512
R = 1024
D = 512
O = 512
R_TILES = R // P
CHUNK = 512
CHUNKS = VIEWS * NEIGH // CHUNK
J_CHUNK = NEIGH // CHUNKS
HALVES = VIEWS // P
K_PASSES = (D + R) // (P * PACK)
W3_BLOCK = 256
W3_LOADS = [1, 1, 2]

HEAD = (0, 1)
GROUPS = ((2, 4, 3), (5, 7, 6))
ON_SCALAR = (4, 7)
PLAIN_FIRST = 5
PLAIN_ORDER = (5, 2, 3, 6, 7, 4)
LAST = PLAIN_ORDER[-1]
PLAIN_AT_END = 8

B3_FACTORS = [(0, 4, 18.0), (4, 5, 4.8), (5, 6, 20.0), (6, 7, 18.0), (7, 8, 6.0)]

WARM_UP = 6

FLOPS = 2 * VIEWS * NEIGH * Q * R + 2 * VIEWS * (D + R) * O


def regroup(engine_copy, dst, src):
    engine_copy(
        out=dst.rearrange("p (c i) t -> p c t i", i=4),
        in_=src.rearrange("p t (c i) -> p c t i", i=4),
    )


def through_scalar(r, c):
    return c == 0 and r != PLAIN_FIRST or c > 1 and r in ON_SCALAR


def share(items, i, n):
    return items[len(items) * i // n : len(items) * (i + 1) // n]


def tile_nonlocalmp_pb_t_kernel(tc, h2, F, W3, b3, Wf, b_f, out):
    nc = tc.nc
    h2_v = h2.rearrange("b (q h) j k -> (b q) h j k", h=HALVES)
    f_v = F.rearrange("b (q h) d -> (b q) h d", h=HALVES)
    out_v = out.rearrange("(p h) o -> p h o", h=HALVES)

    with tc.tile_pool(name="keep", bufs=1) as keep, tc.tile_pool(name="rows", bufs=CHUNKS) as rows, tc.tile_pool(
        name="grp", bufs=3
    ) as grp, tc.tile_pool(name="hand", bufs=4) as hand, tc.psum_pool(
        name="work", bufs=6
    ) as work, tc.psum_pool(name="plain", bufs=2) as plain, tc.manual_schedule():
        ident = keep.tile([P, P], F32)
        w3_raw = [keep.tile([P, PACK, n * W3_BLOCK], BF16, name="w3_raw%d" % i) for i, n in enumerate(W3_LOADS)]
        w3_grp = keep.tile([P, R, PACK], BF16, align_bytes=64)
        w3_words = keep.tile([P, R], U32, align_bytes=64)
        w3_scales = keep.tile([P, R], U8, align_bytes=64)
        h2_words = keep.tile([P, CHUNKS, CHUNK], U32, align_bytes=64)
        h2_scales = keep.tile([P, CHUNKS, CHUNK], U8, align_bytes=64)
        wf_raw = keep.tile([P, K_PASSES, PACK, O], BF16)
        wf_grp = keep.tile([P, K_PASSES, O, PACK], BF16, align_bytes=64)
        wf_words = keep.tile([P, K_PASSES, O], U32, align_bytes=64)
        wf_scales = keep.tile([P, K_PASSES, O], U8, align_bytes=64)
        x_grp = keep.tile([P, K_PASSES, VIEWS, PACK], BF16, align_bytes=64)
        x_words = keep.tile([P, K_PASSES, VIEWS], U32, align_bytes=64)
        x_scales = keep.tile([P, K_PASSES, VIEWS], U8, align_bytes=64)
        f_sb = keep.tile([P, HALVES, D], BF16)
        zeros = keep.tile([P, CHUNK], BF16)
        b3_rows = keep.tile([P, P], BF16)
        b3_rows32 = keep.tile([P, P], F32)
        b3_col = keep.tile([P, R_TILES], F32)
        neg_b3 = keep.tile([P, R_TILES], F32)
        fold_b3 = keep.tile([P, R_TILES], F32)
        bf_all = keep.tile([P, O], BF16)
        folded = keep.tile([P, R_TILES, VIEWS], F32)
        last_sum = keep.tile([P, VIEWS], F32)
        result = keep.tile([P, HALVES, O], F32)
        acc = [keep.tile([P, CHUNK], F32, name="acc%d" % r) for r in range(R_TILES)]

        h2_rows = []

        def load_chunk(c):
            chunk_rows = rows.tile([P, HALVES, J_CHUNK, Q], BF16, name="chunk_rows")
            nc.sync.dma_start(out=chunk_rows[:], in_=h2_v[:, :, J_CHUNK * c : J_CHUNK * (c + 1), :])
            h2_rows.append(chunk_rows)

        def load_w3(i):
            first = sum(W3_LOADS[:i])
            cols = slice(W3_BLOCK * first, W3_BLOCK * (first + W3_LOADS[i]))
            for u in range(2):
                nc.sync.dma_start(
                    out=w3_raw[i][:, 2 * u : 2 * u + 2, :],
                    in_=W3[256 * u : 256 * (u + 1), cols].rearrange("(q e) c -> q e c", e=2),
                )

        nc.vector.memset(zeros[:], 0.0)
        nc.vector.memset(b3_rows[:], 0.0)
        load_chunk(0)
        nc.sync.dma_start(out=b3_rows[0:R_TILES, :], in_=b3.rearrange("(r p) -> r p", p=P))
        load_w3(0)
        load_chunk(1)
        load_w3(1)
        for c in range(2, CHUNKS):
            load_chunk(c)
            if c == CHUNKS // 2:
                load_w3(2)
        nc.sync.dma_start(out=f_sb[:], in_=f_v)
        for u in range(2):
            nc.sync.dma_start(
                out=wf_raw[:, 0, 2 * u : 2 * u + 2, :],
                in_=Wf[256 * u : 256 * (u + 1), :].rearrange("(q e) o -> q e o", e=2),
            )
        for g in range(1, K_PASSES):
            nc.sync.dma_start(
                out=wf_raw[:, g, :, :],
                in_=Wf[512 * g : 512 * (g + 1), :].rearrange("(t p) o -> p t o", p=P),
            )
        nc.sync.dma_start(out=bf_all[:], in_=b_f.partition_broadcast(P))

        make_identity(nc, ident[:])
        nc.gpsimd.memset(acc[PLAIN_FIRST][:, VIEWS:CHUNK], 0.0)

        def transpose_pairs(dst_grp, src_words):
            xt = work.tile([P, 2, HALVES * P], F32, tag="work")
            for h in range(HALVES):
                for u in range(2):
                    nc.tensor.transpose(
                        xt[:, u, P * h : P * (h + 1)], src_words[:, h, P * u : P * (u + 1)], ident[:]
                    )
            nc.scalar.copy(out=dst_grp.bitcast(F32), in_=xt[:].rearrange("p u c -> p c u"))

        chunk_grps = {}

        def transpose_chunk(c):
            chunk_grps[c] = grp.tile([P, CHUNK, PACK], BF16, align_bytes=64, name="chunk_grp")
            words = h2_rows[c][:].bitcast(F32)
            for jj in range(J_CHUNK):
                transpose_pairs(chunk_grps[c][:, VIEWS * jj : VIEWS * (jj + 1), :], words[:, :, jj, :])

        def quantise_chunk(c):
            nc.vector.quantize_mx(
                out=h2_words[:, c, :].bitcast(FP8X4),
                scales=h2_scales[:, c, :],
                in_=chunk_grps[c][:].rearrange("p c t -> p (c t)"),
            )

        def regroup_w3(engine_copy, r, tiles):
            i = min(P * r // W3_BLOCK, len(W3_LOADS) - 1)
            first = P * r - W3_BLOCK * i
            raw_cols = slice(first, first + P * tiles)
            regroup(engine_copy, w3_grp[:, P * r : P * (r + tiles), :], w3_raw[i][:, :, raw_cols])

        def quantise_w3(block):
            cols = slice(W3_BLOCK * block, W3_BLOCK * (block + 1))
            nc.vector.quantize_mx(
                out=w3_words[:, cols].bitcast(FP8X4),
                scales=w3_scales[:, cols],
                in_=w3_grp[:, cols, :].rearrange("p c t -> p (c t)"),
            )

        def message_pass(dst, r, c, cols, start, stop):
            tile_cols = slice(P * r, P * (r + 1))
            nc.tensor.matmul_mx(
                out=dst,
                lhsT=w3_words[:, tile_cols].bitcast(FP8X4),
                lhsT_scale=w3_scales[:, tile_cols],
                rhs=h2_words[:, c, cols].bitcast(FP8X4),
                rhs_scale=h2_scales[:, c, cols],
                start=start,
                stop=stop,
            )

        def relu_sum(r, c):
            bank = work.tile([P, CHUNK], F32, tag="work")
            message_pass(bank[:], r, c, slice(0, CHUNK), True, True)
            if through_scalar(r, c):
                if c == 0:
                    nc.scalar.activation(out=acc[r][:], in_=bank[:], func=ACT.Relu, bias=b3_col[:, r : r + 1])
                else:
                    relu_sb = hand.tile([P, CHUNK], F32, tag="hand")
                    nc.scalar.activation(out=relu_sb[:], in_=bank[:], func=ACT.Relu, bias=b3_col[:, r : r + 1])
                    nc.gpsimd.tensor_tensor(out=acc[r][:], in0=acc[r][:], in1=relu_sb[:], op=ALU.add)
            else:
                nc.vector.scalar_tensor_tensor(
                    out=acc[r][:],
                    in0=bank[:],
                    scalar=neg_b3[:, r : r + 1],
                    in1=acc[r][:],
                    op0=ALU.max,
                    op1=ALU.add,
                )

        plain_sums = {}

        def plain_pass(r, j, views):
            if r not in plain_sums:
                plain_sums[r] = plain.tile([P, CHUNK], F32, name="plain_sum")
            start = VIEWS * (j % J_CHUNK)
            message_pass(
                plain_sums[r][:, views],
                r,
                j // J_CHUNK,
                slice(start + views.start, start + views.stop),
                j == 0,
                j == NEIGH - 1,
            )

        def fold(r):
            nc.vector.scalar_tensor_tensor(
                out=folded[:, r, :],
                in0=acc[r][:, 0:VIEWS],
                scalar=fold_b3[:, r : r + 1],
                in1=acc[r][:, VIEWS:CHUNK],
                op0=ALU.add,
                op1=ALU.add,
            )

        def add_plain_sum(r, dst):
            nc.vector.scalar_tensor_tensor(
                out=dst, in0=plain_sums[r][:, 0:VIEWS], scalar=0.25, in1=dst, op0=ALU.mult, op1=ALU.add
            )

        def finish(r):
            plain_sb = hand.tile([P, VIEWS], F32, tag="plain_sb")
            nc.scalar.activation(
                out=plain_sb[:],
                in_=plain_sums[r][:, 0:VIEWS],
                func=ACT.Identity,
                scale=0.25,
                bias=fold_b3[:, r : r + 1],
            )
            nc.gpsimd.tensor_tensor(
                out=folded[:, r, :], in0=acc[r][:, 0:VIEWS], in1=acc[r][:, VIEWS:CHUNK], op=ALU.add
            )
            nc.gpsimd.tensor_tensor(out=folded[:, r, :], in0=folded[:, r, :], in1=plain_sb[:], op=ALU.add)

        def regroup_wf(piece):
            g = piece // 4
            cols = slice((O // 4) * (piece % 4), (O // 4) * (piece % 4 + 1))
            regroup(nc.scalar.copy, wf_grp[:, g, cols, :], wf_raw[:, g, :, cols])

        def quantise_wf(g):
            nc.vector.quantize_mx(
                out=wf_words[:, g, :].bitcast(FP8X4),
                scales=wf_scales[:, g, :],
                in_=wf_grp[:, g, :, :].rearrange("p c t -> p (c t)"),
            )

        def regroup_x(g):
            for h in range(HALVES):
                cols = slice(P * h, P * (h + 1))
                src = folded[:, PACK * (g - 1) : PACK * g, cols].rearrange("p t c -> p c t")
                if h == 0:
                    nc.vector.tensor_scalar(
                        out=x_grp[:, g, cols, :], in0=src, scalar1=0.8, scalar2=None, op0=ALU.mult
                    )
                else:
                    nc.scalar.activation(out=x_grp[:, g, cols, :], in_=src, func=ACT.Copy, scale=0.8)

        def quantise_x(g, cols):
            nc.vector.quantize_mx(
                out=x_words[:, g, cols].bitcast(FP8X4),
                scales=x_scales[:, g, cols],
                in_=x_grp[:, g, cols, :].rearrange("p c t -> p (c t)"),
            )

        def fusion_pass(fused, h, g):
            nc.tensor.matmul_mx(
                out=fused[:],
                lhsT=x_words[:, g, P * h : P * (h + 1)].bitcast(FP8X4),
                lhsT_scale=x_scales[:, g, P * h : P * (h + 1)],
                rhs=wf_words[:, g, :].bitcast(FP8X4),
                rhs_scale=wf_scales[:, g, :],
                start=(g == 0),
                stop=(g == K_PASSES - 1),
            )

        for i in range(WARM_UP):
            idle_bank = work.tile([P, CHUNK], F32, tag="work")
            nc.tensor.matmul(out=idle_bank[:], lhsT=zeros[:, 0:P], rhs=zeros[:], start=True, stop=True)
        transpose_chunk(0)
        transpose_chunk(1)
        regroup_w3(nc.vector.tensor_copy, 0, 2)
        nc.gpsimd.tensor_copy(out=b3_rows32[:], in_=b3_rows[:])
        b3_t = work.tile([P, CHUNK], F32, tag="work")
        nc.tensor.transpose(b3_t[:, 0:P], b3_rows32[:], ident[:])
        quantise_w3(0)
        quantise_chunk(0)
        nc.vector.tensor_copy(out=b3_col[:], in_=b3_t[:, 0:R_TILES])
        nc.vector.tensor_scalar(out=neg_b3[:], in0=b3_col[:], scalar1=-1.0, scalar2=None, op0=ALU.mult)
        for c in range(CHUNKS):
            for r in HEAD:
                relu_sum(r, c)
                if r == 0 and c + 1 < CHUNKS:
                    quantise_chunk(c + 1)
            for r in HEAD:
                for jj in range(J_CHUNK):
                    plain_pass(r, J_CHUNK * c + jj, slice(0, VIEWS))
            if c + 2 < CHUNKS:
                transpose_chunk(c + 2)
            if c + 2 == CHUNKS:
                transpose_pairs(x_grp[:, 0, :, :], f_sb[:].bitcast(F32))
            if 1 <= c <= 6:
                regroup_w3(nc.scalar.copy, c + 1, 1)
            if c in (4, 6):
                quantise_w3(c // 2 - 1)
            if c == 1:
                for first, last, factor in B3_FACTORS:
                    nc.scalar.activation(
                        out=fold_b3[:, first:last], in_=b3_col[:, first:last], func=ACT.Copy, scale=factor
                    )

        for r in HEAD:
            finish(r)

        order = [(r, c) for group in GROUPS for c in range(CHUNKS) for r in group]
        passes = [(r, j, slice(0, VIEWS)) for r in PLAIN_ORDER[:-1] for j in range(NEIGH)]
        last_passes = [[(LAST, j, slice(P * h, P * (h + 1))) for j in range(NEIGH)] for h in range(HALVES)]
        along = len(passes) - PLAIN_AT_END
        closed = []
        for i, (r, c) in enumerate(order):
            relu_sum(r, c)
            ready = closed
            closed = []
            for r_plain in ready:
                if r_plain == PLAIN_FIRST:
                    nc.scalar.activation(
                        out=acc[r_plain][:, 0:VIEWS],
                        in_=plain_sums[r_plain][:, 0:VIEWS],
                        func=ACT.Copy,
                        scale=0.25,
                    )
                else:
                    add_plain_sum(r_plain, acc[r_plain][:, 0:VIEWS])
            for r_plain, j, views in share(passes[:along], i, len(order)):
                plain_pass(r_plain, j, views)
                if j == NEIGH - 1:
                    closed.append(r_plain)
            if (r, c) == (3, 3):
                quantise_x(0, slice(0, VIEWS))
            if r == 4:
                regroup_wf(c)
            if r == 7 and c < 4:
                regroup_wf(8 + c)
            if (r, c) == (7, 1):
                nc.gpsimd.tensor_tensor(
                    out=folded[:, LAST, :], in0=acc[LAST][:, 0:VIEWS], in1=acc[LAST][:, VIEWS:CHUNK], op=ALU.add
                )
            if (r, c) == (3, 4):
                quantise_wf(0)
            if (r, c) == (5, 1):
                quantise_wf(1)
            if (r, c) == (5, 5):
                quantise_wf(2)
            if (r, c) == (5, 2):
                fold(2)
            if (r, c) == (5, 4):
                fold(3)
            if (r, c) == (3, 5):
                quantise_w3(3)
            if (r, c) == (6, 5):
                regroup_x(1)
            if (r, c) == (6, 6):
                quantise_x(1, slice(0, VIEWS))

        fold(5)
        fold(6)
        for r_plain, j, views in passes[along:]:
            plain_pass(r_plain, j, views)
        nc.scalar.activation(
            out=last_sum[:], in_=folded[:, LAST, :], func=ACT.Identity, scale=0.8, bias=fold_b3[:, LAST : LAST + 1]
        )
        finish(7)
        for r_plain, j, views in last_passes[0]:
            plain_pass(r_plain, j, views)
        fused = []
        for h in range(HALVES):
            fused.append(work.tile([P, O], F32, tag="work", name="fused"))
            fusion_pass(fused[h], h, 0)
            fusion_pass(fused[h], h, 1)
        for r_plain, j, views in last_passes[1]:
            plain_pass(r_plain, j, views)
        regroup_x(2)
        for h in range(HALVES):
            cols = slice(P * h, P * (h + 1))
            nc.vector.scalar_tensor_tensor(
                out=x_grp[:, 2, cols, LAST % PACK],
                in0=plain_sums[LAST][:, cols],
                scalar=0.2,
                in1=last_sum[:, cols],
                op0=ALU.mult,
                op1=ALU.add,
            )
            quantise_x(2, cols)
            fusion_pass(fused[h], h, 2)
        for h in range(HALVES):
            nc.vector.tensor_tensor(out=result[:, h, :], in0=fused[h][:], in1=bf_all[:], op=ALU.add)
            nc.sync.dma_start(out=out_v[:, h, :], in_=result[:, h, :])
